import numpy as np
import ml_dtypes


def mxq(x, axis, fmt="e4m3"):
    dtype, down = {"e4m3": (ml_dtypes.float8_e4m3fn, 7), "e5m2": (ml_dtypes.float8_e5m2, 14)}[fmt]
    v = np.moveaxis(np.asarray(x, np.float32).astype(ml_dtypes.bfloat16).astype(np.float64), axis, -1)
    blocks = v.reshape(v.shape[:-1] + (-1, 32))
    amax = np.abs(blocks).max(-1, keepdims=True)
    byte = np.maximum(np.where(amax > 0, np.frexp(amax)[1] - 1 + 127, 0) - down, 1)
    scale = np.exp2(byte - 127.0)
    codes = (blocks / scale).astype(np.float32).astype(dtype).astype(np.float64)
    return np.moveaxis((codes * scale).reshape(v.shape), -1, axis)


WIDE = False


def mx_kscale(k):
    if not WIDE:
        return np.ones(k)
    levels = np.array([10, -10, 5, -5, 0])
    a = np.random.permutation(np.resize(levels, k // 512 * 4)).reshape(k // 512, 4)
    idx = np.arange(k)
    return np.exp2(a[idx // 512, idx % 128 // 32])


BF16 = ml_dtypes.bfloat16


def bf(x):
    return np.asarray(x, np.float32).astype(BF16)


def f64(x):
    return np.asarray(x).astype(np.float64)


E2M1 = np.array([0.0, 0.5, 1.0, 1.5, 2.0, 3.0, 4.0, 6.0, -0.0, -0.5, -1.0, -1.5, -2.0, -3.0, -4.0, -6.0])


def pack_weight(w, fmt):
    k, n = w.shape
    w = f64(bf(w)).reshape(k // 32, 32, n)
    amax = np.abs(w).max(1)
    if fmt == "e4m3":
        byte = np.frexp(amax)[1] - 1 + 127 - 7
    else:
        mant, ex = np.frexp(amax / 6.0)
        byte = np.where(mant > 0.5, ex, ex - 1) + 127
    byte = np.clip(np.where(amax > 0, byte, 1), 1, 254)
    scaled = (w * np.exp2(127.0 - byte)[:, None, :]).reshape(k, n).astype(np.float32)
    by_word = np.ascontiguousarray(scaled.reshape(k // 512, 128, 4, n).transpose(0, 1, 3, 2))
    if fmt == "e4m3":
        words = by_word.astype(ml_dtypes.float8_e4m3fn).view(np.uint8)
    else:
        c = by_word.astype(ml_dtypes.float4_e2m1fn).view(np.uint8) & 0xF
        words = c[..., 0::2] | (c[..., 1::2] << 4)
    return np.ascontiguousarray(words), np.ascontiguousarray(byte.astype(np.uint8).reshape(k // 512, 16, n))


def unpack_weight(words, scales, fmt):
    g, p, n, _ = words.shape
    if fmt == "e4m3":
        vals = np.ascontiguousarray(words).view(ml_dtypes.float8_e4m3fn).astype(np.float64)
    else:
        nib = np.empty((g, p, n, 4), np.uint8)
        nib[..., 0::2] = words & 0xF
        nib[..., 1::2] = words >> 4
        vals = E2M1[nib]
    vals = vals * np.repeat(np.exp2(scales.astype(np.float64) - 127.0), 8, axis=1)[..., None]
    return vals.transpose(0, 1, 3, 2).reshape(g * 512, n)

def pack4(w):
    words, scales = pack_weight(w, "e2m1")
    return words.reshape(words.shape[0], 128, -1), scales


def unpack4(words, scales):
    return unpack_weight(words.reshape(words.shape[0], 128, -1, 2), scales, "e2m1")


B, S, D = 2, 1024, 1024
EPS = 1e-8


def layer_norm(v, w, b):
    mu = v.mean(-1, keepdims=True)
    var = ((v - mu) ** 2).mean(-1, keepdims=True)
    return (v - mu) / np.sqrt(var + EPS) * w + b


def setup_inputs():
    s = mx_kscale(D)
    xr = np.random.standard_normal((B, S, D)) + np.random.uniform(-1.2, 1.2, (B, S, 1))
    xi = np.random.standard_normal((B, S, D)) + np.random.uniform(-1.2, 1.2, (B, S, 1))
    words, scales = pack4(np.random.standard_normal((D, D)) / np.sqrt(D) / s[:, None])
    return {"x_real": bf(xr * s), "x_imag": bf(xi * s),
            "phase_matrix_words": words, "phase_matrix_scales": scales,
            "coherence_factor": bf(np.random.uniform(0.35, 0.5, 1)),
            "ln_weight": bf(1.0 + 0.1 * np.random.standard_normal(D)),
            "ln_bias": bf(0.3 * np.random.standard_normal(D))}


def reference(x_real, x_imag, phase_matrix_words, phase_matrix_scales, coherence_factor, ln_weight, ln_bias):
    xr, xi = f64(x_real), f64(x_imag)
    a, b = xr + EPS, xi + EPS
    r = np.sqrt(a * a + b * b)
    sc = (a / r).sum(-1, keepdims=True)
    ss = (b / r).sum(-1, keepdims=True)
    coherence = (sc * sc + ss * ss) / (D * D)
    p = mxq(xr, 2, "e4m3") @ unpack4(phase_matrix_words, phase_matrix_scales)
    p = p * f64(coherence_factor) * (1.0 - coherence)
    c, sn = np.cos(p), np.sin(p)
    new_real = xr * c - xi * sn
    new_imag = xr * sn + xi * c
    norm = np.sqrt(new_real ** 2 + new_imag ** 2 + EPS)
    new_real = new_real / norm
    new_imag = new_imag / norm
    w, bb = f64(ln_weight), f64(ln_bias)
    return (layer_norm(new_real, w, bb), layer_norm(new_imag, w, bb))

@@ -1,0 +1,382 @@
+import math
+from contextlib import ExitStack
+
+import concourse.mybir as mybir
+from concourse.masks import make_identity
+
+F32 = mybir.dt.float32
+BF16 = mybir.dt.bfloat16
+I32 = mybir.dt.int32
+U32 = mybir.dt.uint32
+U8 = mybir.dt.uint8
+FP8X4 = mybir.dt.float8_e4m3fn_x4
+FP4X4 = mybir.dt.float4_e2m1fn_x4
+ACT = mybir.ActivationFunctionType
+ALU = mybir.AluOpType
+
+P = 128
+D = 1024
+ROWS = 2 * 1024
+TILES = ROWS // P
+HALF = 512
+BANKS = D // HALF
+K_PASSES = D // (4 * P)
+EPS = 1e-8
+ROUND_MAGIC = 12582912.0
+LN_LAG = 3
+
+FLOPS = 2 * ROWS * D * D
+
+
+def tile_quantumcoherencelayer_kernel(
+    tc,
+    x_real,
+    x_imag,
+    phase_matrix_words,
+    phase_matrix_scales,
+    coherence_factor,
+    ln_weight,
+    ln_bias,
+    out_0,
+    out_1,
+):
+    nc = tc.nc
+    xr_rows = x_real.flatten_outer_dims().rearrange("(p i) d -> p i d", i=TILES)
+    xi_rows = x_imag.flatten_outer_dims().rearrange("(p i) d -> p i d", i=TILES)
+    out_rows = [
+        o.flatten_outer_dims().rearrange("(p i) d -> p i d", i=TILES) for o in (out_0, out_1)
+    ]
+
+    with tc.manual_schedule(), ExitStack() as whole:
+        keep = whole.enter_context(tc.tile_pool(name="keep", bufs=1))
+        tiny = whole.enter_context(tc.tile_pool(name="tiny", bufs=6))
+
+        unit = [keep.tile([P, 2, D], F32, name="unit%d" % i) for i in range(TILES)]
+        x_codes = [
+            keep.tile([P, K_PASSES * P], U32, name="x_codes%d" % i, align_bytes=64)
+            for i in range(TILES)
+        ]
+        x_scales = [
+            keep.tile([P, K_PASSES * P], U8, name="x_scales%d" % i, align_bytes=64)
+            for i in range(TILES)
+        ]
+        turns_gain = [keep.tile([P, 1], F32, name="turns_gain%d" % i) for i in range(TILES)]
+
+        x_tiles = {}
+        part1 = {}
+
+        with tc.tile_pool(name="x_in", bufs=3) as x_in, tc.tile_pool(
+            name="work1", bufs=2
+        ) as work1, tc.psum_pool(name="xt_psum", bufs=2) as xt_psum:
+
+            def load(i):
+                xri = x_in.tile([P, 2, D], BF16, name="xri")
+                nc.sync.dma_start(out=xri[:, 0, :], in_=xr_rows[:, i, :])
+                nc.sync.dma_start(out=xri[:, 1, :], in_=xi_rows[:, i, :])
+                x_tiles[i] = xri
+
+            load(0)
+            load(1)
+
+            ident = keep.tile([P, P], F32, name="ident")
+            make_identity(nc, ident[:])
+            ones = keep.tile([P, 1], F32, name="ones")
+            nc.vector.memset(ones[:], 1.0)
+            eps = keep.tile([P, 1], F32, name="eps")
+            nc.vector.tensor_scalar(
+                out=eps[:], in0=ones[:], scalar1=EPS, scalar2=None, op0=ALU.mult
+            )
+            quarter_turn = keep.tile([P, 1], F32, name="quarter_turn")
+            nc.vector.tensor_scalar(
+                out=quarter_turn[:], in0=ones[:], scalar1=math.pi / 2, scalar2=None, op0=ALU.mult
+            )
+            magic = keep.tile([P, 1], F32, name="magic")
+            nc.vector.memset(magic[:], ROUND_MAGIC)
+            minus_magic = keep.tile([P, 1], F32, name="minus_magic")
+            nc.vector.memset(minus_magic[:], -ROUND_MAGIC)
+            minus_half = keep.tile([P, 2], F32, name="minus_half")
+            nc.vector.memset(minus_half[:], -0.5)
+
+            w_words = keep.tile([P, K_PASSES, 2 * D], U8, name="w_words", align_bytes=64)
+            w_scales = keep.tile([P, K_PASSES, D], U8, name="w_scales", align_bytes=64)
+            nc.vector.memset(w_scales[:].bitcast(I32), 0)
+            factor = keep.tile([P, 1], BF16, name="factor")
+            nc.sync.dma_start(out=factor[:], in_=coherence_factor.partition_broadcast(P))
+            for quadrant in range(4):
+                nc.sync.dma_start(
+                    out=w_scales[32 * quadrant : 32 * quadrant + 4, :, :].bitcast(I32),
+                    in_=phase_matrix_scales[:, 4 * quadrant : 4 * quadrant + 4, :]
+                    .rearrange("g r n -> r g n")
+                    .bitcast(I32),
+                )
+            nc.sync.dma_start(
+                out=w_words[:].bitcast(I32),
+                in_=phase_matrix_words.rearrange("g p n -> p g n").bitcast(I32),
+            )
+            full_gain = keep.tile([P, 1], F32, name="full_gain")
+            nc.vector.tensor_scalar(
+                out=full_gain[:],
+                in0=factor[:],
+                scalar1=1.0 / (2.0 * math.pi),
+                scalar2=None,
+                op0=ALU.mult,
+            )
+            gain_slope = keep.tile([P, 1], F32, name="gain_slope")
+            nc.vector.tensor_scalar(
+                out=gain_slope[:],
+                in0=factor[:],
+                scalar1=-1.0 / (2.0 * math.pi * D * D),
+                scalar2=None,
+                op0=ALU.mult,
+            )
+
+            def squares_and_words(i):
+                xri = x_tiles[i]
+                shifted_sq = work1.tile([P, 2, D], F32, name="shifted_sq")
+                nc.scalar.activation(out=shifted_sq[:], in_=xri[:], func=ACT.Square, bias=eps[:])
+                plain_sq = work1.tile([P, 2, D], F32, name="plain_sq")
+                nc.scalar.activation(out=plain_sq[:], in_=xri[:], func=ACT.Square)
+                words = xri[:, 0, :].bitcast(F32)
+                xt = xt_psum.tile([P, 2 * K_PASSES, P], F32, name="xt")
+                for g in range(K_PASSES):
+                    for u in range(2):
+                        nc.tensor.transpose(
+                            xt[:, 2 * g + u, :], words[:, 256 * g + u : 256 * (g + 1) : 2], ident[:]
+                        )
+                grouped = work1.tile([P, K_PASSES, P, 2], F32, name="grouped", align_bytes=64)
+                nc.scalar.copy(out=grouped[:], in_=xt[:].rearrange("p (g u) r -> p g r u", u=2))
+                moduli = work1.tile([P, 2, D], F32, name="moduli")
+                nc.vector.tensor_tensor(
+                    out=moduli[:, 0, :], in0=shifted_sq[:, 0, :], in1=shifted_sq[:, 1, :], op=ALU.add
+                )
+                nc.vector.scalar_tensor_tensor(
+                    out=moduli[:, 1, :],
+                    in0=plain_sq[:, 0, :],
+                    scalar=EPS,
+                    in1=plain_sq[:, 1, :],
+                    op0=ALU.add,
+                    op1=ALU.add,
+                )
+                part1[i] = (grouped, moduli)
+
+            def coherence_and_unit(i):
+                xri = x_tiles[i]
+                grouped, moduli = part1[i]
+                nc.scalar.activation(out=moduli[:], in_=moduli[:], func=ACT.Abs_reciprocal_sqrt)
+                sums = tiny.tile([P, 2], F32, name="sums")
+                for part in range(2):
+                    unread = work1.tile([P, D], F32, name="unread")
+                    nc.vector.scalar_tensor_tensor(
+                        out=unread[:],
+                        in0=xri[:, part, :],
+                        scalar=EPS,
+                        in1=moduli[:, 0, :],
+                        op0=ALU.add,
+                        op1=ALU.mult,
+                        accum_out=sums[:, part : part + 1],
+                    )
+                nc.vector.tensor_tensor(
+                    out=unit[i][:],
+                    in0=xri[:],
+                    in1=moduli[:, 1:2, :].to_broadcast([P, 2, D]),
+                    op=ALU.mult,
+                )
+                nc.vector.quantize_mx(
+                    out=x_codes[i][:].bitcast(FP8X4),
+                    scales=x_scales[i][:],
+                    in_=grouped[:].rearrange("p g r u -> p (g r u)").bitcast(BF16),
+                )
+                sums_sq = tiny.tile([P, 2], F32, name="sums_sq")
+                nc.gpsimd.tensor_tensor(out=sums_sq[:], in0=sums[:], in1=sums[:], op=ALU.mult)
+                length_sq = tiny.tile([P, 1], F32, name="length_sq")
+                nc.gpsimd.tensor_tensor(
+                    out=length_sq[:], in0=sums_sq[:, 0:1], in1=sums_sq[:, 1:2], op=ALU.add
+                )
+                nc.gpsimd.tensor_scalar(
+                    out=turns_gain[i][:],
+                    in0=length_sq[:],
+                    scalar1=gain_slope[:],
+                    scalar2=full_gain[:],
+                    op0=ALU.mult,
+                    op1=ALU.add,
+                )
+
+            for step in range(TILES + 1):
+                if step < TILES:
+                    squares_and_words(step)
+                if step >= 1:
+                    coherence_and_unit(step - 1)
+                if step + 2 < TILES:
+                    load(step + 2)
+
+        with tc.tile_pool(name="work2", bufs=2, reuse_waits="tile") as work2, tc.psum_pool(
+            name="product_psum", bufs=3
+        ) as product_psum:
+            ln_w = work2.tile([P, D], BF16, name="ln_w", bufs=1)
+            nc.sync.dma_start(out=ln_w[:], in_=ln_weight.partition_broadcast(P))
+            ln_b = work2.tile([P, D], BF16, name="ln_b", bufs=1)
+            nc.sync.dma_start(out=ln_b[:], in_=ln_bias.partition_broadcast(P))
+
+            products = {}
+            angles = {}
+            phasors = {}
+            totals = {}
+            moments = {}
+
+            def multiply(i):
+                product = product_psum.tile([P, BANKS, HALF], F32, name="product")
+                for b in range(BANKS):
+                    for g in range(K_PASSES):
+                        nc.tensor.matmul_mx(
+                            out=product[:, b, :],
+                            lhsT=x_codes[i][:, P * g : P * (g + 1)].bitcast(FP8X4),
+                            lhsT_scale=x_scales[i][:, P * g : P * (g + 1)],
+                            rhs=w_words[:, g, 2 * HALF * b : 2 * HALF * (b + 1)].bitcast(FP4X4),
+                            rhs_scale=w_scales[:, g, HALF * b : HALF * (b + 1)],
+                            start=(g == 0),
+                            stop=(g == K_PASSES - 1),
+                        )
+                products[i] = product
+
+            def reduce_angle(i):
+                product = products[i]
+                whole_turns = work2.tile([P, BANKS, HALF], F32, name="whole_turns")
+                for b in range(BANKS):
+                    nc.scalar.activation(
+                        out=whole_turns[:, b, :],
+                        in_=product[:, b, :],
+                        func=ACT.Identity,
+                        scale=turns_gain[i][:],
+                        bias=magic[:],
+                    )
+                nc.scalar.activation(
+                    out=whole_turns[:], in_=whole_turns[:], func=ACT.Identity, bias=minus_magic[:]
+                )
+                frac = work2.tile([P, BANKS, HALF], F32, name="frac")
+                for b in range(BANKS):
+                    nc.vector.scalar_tensor_tensor(
+                        out=frac[:, b, :],
+                        in0=product[:, b, :],
+                        scalar=turns_gain[i][:],
+                        in1=whole_turns[:, b, :],
+                        op0=ALU.mult,
+                        op1=ALU.subtract,
+                    )
+                angles[i] = (frac, whole_turns)
+
+            def sine_and_cosine(i):
+                frac, abs_frac = angles[i]
+                nc.scalar.activation(out=abs_frac[:], in_=frac[:], func=ACT.Abs)
+                phasor = work2.tile([P, 2, D], F32, name="phasor")
+                nc.scalar.activation(
+                    out=phasor[:, 0, :],
+                    in_=abs_frac[:].rearrange("p b n -> p (b n)"),
+                    func=ACT.Sin,
+                    scale=-2.0 * math.pi,
+                    bias=quarter_turn[:],
+                )
+                nc.scalar.activation(
+                    out=phasor[:, 1, :],
+                    in_=frac[:].rearrange("p b n -> p (b n)"),
+                    func=ACT.Sin,
+                    scale=2.0 * math.pi,
+                )
+                phasors[i] = phasor
+
+            def rotate(i):
+                phasor = phasors[i]
+                by_sin = work2.tile([P, 2, D], F32, name="by_sin")
+                nc.vector.tensor_tensor(
+                    out=by_sin[:],
+                    in0=unit[i][:],
+                    in1=phasor[:, 1:2, :].to_broadcast([P, 2, D]),
+                    op=ALU.mult,
+                )
+                nc.vector.tensor_tensor(
+                    out=unit[i][:],
+                    in0=unit[i][:],
+                    in1=phasor[:, 0:1, :].to_broadcast([P, 2, D]),
+                    op=ALU.mult,
+                )
+                total = tiny.tile([P, 2], F32, name="total")
+                nc.vector.scalar_tensor_tensor(
+                    out=unit[i][:, 0, :],
+                    in0=unit[i][:, 0, :],
+                    scalar=1.0,
+                    in1=by_sin[:, 1, :],
+                    op0=ALU.mult,
+                    op1=ALU.subtract,
+                    accum_out=total[:, 0:1],
+                )
+                nc.vector.scalar_tensor_tensor(
+                    out=unit[i][:, 1, :],
+                    in0=unit[i][:, 1, :],
+                    scalar=1.0,
+                    in1=by_sin[:, 0, :],
+                    op0=ALU.mult,
+                    op1=ALU.add,
+                    accum_out=total[:, 1:2],
+                )
+                totals[i] = total
+
+            def row_moments(i):
+                total_sq = tiny.tile([P, 2], F32, name="total_sq")
+                for part in range(2):
+                    unread = work2.tile([P, D], BF16, name="unread_sq")
+                    nc.scalar.activation(
+                        out=unread[:],
+                        in_=unit[i][:, part, :],
+                        func=ACT.Square,
+                        accum_out=total_sq[:, part : part + 1],
+                    )
+                mean = tiny.tile([P, 2], F32, name="mean")
+                nc.gpsimd.tensor_scalar(
+                    out=mean[:], in0=totals[i][:], scalar1=1.0 / D, scalar2=0.0, op0=ALU.mult, op1=ALU.add
+                )
+                spread = tiny.tile([P, 2], F32, name="spread")
+                nc.gpsimd.tensor_scalar(
+                    out=spread[:], in0=total_sq[:], scalar1=1.0 / D, scalar2=EPS, op0=ALU.mult, op1=ALU.add
+                )
+                mean_sq = tiny.tile([P, 2], F32, name="mean_sq")
+                nc.gpsimd.tensor_tensor(out=mean_sq[:], in0=mean[:], in1=mean[:], op=ALU.mult)
+                nc.gpsimd.tensor_tensor(out=spread[:], in0=spread[:], in1=mean_sq[:], op=ALU.subtract)
+                rstd = tiny.tile([P, 2], F32, name="rstd")
+                nc.gpsimd.tensor_tensor(out=rstd[:], in0=spread[:], in1=minus_half[:], op=ALU.pow)
+                moments[i] = (mean, rstd)
+
+            def layer_norms(i):
+                mean, rstd = moments[i]
+                for part in range(2):
+                    normed = work2.tile([P, D], F32, name="normed", bufs=4)
+                    nc.vector.scalar_tensor_tensor(
+                        out=normed[:],
+                        in0=unit[i][:, part, :],
+                        scalar=mean[:, part : part + 1],
+                        in1=ln_w[:],
+                        op0=ALU.subtract,
+                        op1=ALU.mult,
+                    )
+                    nc.vector.scalar_tensor_tensor(
+                        out=normed[:],
+                        in0=normed[:],
+                        scalar=rstd[:, part : part + 1],
+                        in1=ln_b[:],
+                        op0=ALU.mult,
+                        op1=ALU.add,
+                    )
+                    nc.sync.dma_start(out=out_rows[part][:, i, :], in_=normed[:])
+
+            multiply(0)
+            for step in range(TILES + LN_LAG):
+                if step + 1 < TILES:
+                    multiply(step + 1)
+                if step < TILES:
+                    reduce_angle(step)
+                if 0 <= step - 1 < TILES:
+                    sine_and_cosine(step - 1)
+                if 0 <= step - LN_LAG < TILES:
+                    layer_norms(step - LN_LAG)
+                if 0 <= step - 1 < TILES:
+                    rotate(step - 1)
+                if 0 <= step - 2 < TILES:
+                    row_moments(step - 2)

@@ -23,7 +23,7 @@ BANKS = D // HALF
 K_PASSES = D // (4 * P)
 EPS = 1e-8
 ROUND_MAGIC = 12582912.0
-LN_LAG = 3
+LN_LAG = 4
 
 FLOPS = 2 * ROWS * D * D
 
@@ -210,17 +210,31 @@ def tile_quantumcoherencelayer_kernel(
                     load(step + 2)
 
         with tc.tile_pool(name="work2", bufs=2, reuse_waits="tile") as work2, tc.psum_pool(
-            name="product_psum", bufs=3
-        ) as product_psum:
-            ln_w = work2.tile([P, D], BF16, name="ln_w", bufs=1)
-            nc.sync.dma_start(out=ln_w[:], in_=ln_weight.partition_broadcast(P))
-            ln_b = work2.tile([P, D], BF16, name="ln_b", bufs=1)
-            nc.sync.dma_start(out=ln_b[:], in_=ln_bias.partition_broadcast(P))
+            name="affine_psum", bufs=1
+        ) as affine_psum, tc.psum_pool(name="product_psum", bufs=2) as product_psum:
+            ln_rows = work2.tile([P, 2, D], BF16, name="ln_rows", bufs=1)
+            nc.vector.memset(ln_rows[:], 0.0)
+            nc.sync.dma_start(out=ln_rows[0:1, 0, :], in_=ln_weight.rearrange("(o d) -> o d", o=1))
+            nc.sync.dma_start(out=ln_rows[0:1, 1, :], in_=ln_bias.rearrange("(o d) -> o d", o=1))
+            first_row = work2.tile([P, P], BF16, name="first_row", bufs=1)
+            nc.vector.memset(first_row[:], 0.0)
+            nc.vector.memset(first_row[0:1, :], 1.0)
+            affine = affine_psum.tile([P, 2, BANKS, HALF], F32, name="affine")
+            for which in range(2):
+                for b in range(BANKS):
+                    nc.tensor.matmul(
+                        out=affine[:, which, b, :],
+                        lhsT=first_row[:],
+                        rhs=ln_rows[:, which, HALF * b : HALF * (b + 1)],
+                        start=True,
+                        stop=True,
+                    )
 
             products = {}
             angles = {}
             phasors = {}
             totals = {}
+            squares = {}
             moments = {}
 
             def multiply(i):
@@ -269,24 +283,24 @@ def tile_quantumcoherencelayer_kernel(
                 nc.scalar.activation(out=abs_frac[:], in_=frac[:], func=ACT.Abs)
                 phasor = work2.tile([P, 2, D], F32, name="phasor")
                 nc.scalar.activation(
+                    out=phasor[:, 1, :],
+                    in_=frac[:].rearrange("p b n -> p (b n)"),
+                    func=ACT.Sin,
+                    scale=2.0 * math.pi,
+                )
+                nc.scalar.activation(
                     out=phasor[:, 0, :],
                     in_=abs_frac[:].rearrange("p b n -> p (b n)"),
                     func=ACT.Sin,
                     scale=-2.0 * math.pi,
                     bias=quarter_turn[:],
                 )
-                nc.scalar.activation(
-                    out=phasor[:, 1, :],
-                    in_=frac[:].rearrange("p b n -> p (b n)"),
-                    func=ACT.Sin,
-                    scale=2.0 * math.pi,
-                )
                 phasors[i] = phasor
 
             def rotate(i):
                 phasor = phasors[i]
                 by_sin = work2.tile([P, 2, D], F32, name="by_sin")
-                nc.vector.tensor_tensor(
+                nc.gpsimd.tensor_tensor(
                     out=by_sin[:],
                     in0=unit[i][:],
                     in1=phasor[:, 1:2, :].to_broadcast([P, 2, D]),
@@ -319,7 +333,7 @@ def tile_quantumcoherencelayer_kernel(
                 )
                 totals[i] = total
 
-            def row_moments(i):
+            def sums_of_squares(i):
                 total_sq = tiny.tile([P, 2], F32, name="total_sq")
                 for part in range(2):
                     unread = work2.tile([P, D], BF16, name="unread_sq")
@@ -329,13 +343,16 @@ def tile_quantumcoherencelayer_kernel(
                         func=ACT.Square,
                         accum_out=total_sq[:, part : part + 1],
                     )
+                squares[i] = total_sq
+
+            def row_moments(i):
                 mean = tiny.tile([P, 2], F32, name="mean")
                 nc.gpsimd.tensor_scalar(
                     out=mean[:], in0=totals[i][:], scalar1=1.0 / D, scalar2=0.0, op0=ALU.mult, op1=ALU.add
                 )
                 spread = tiny.tile([P, 2], F32, name="spread")
                 nc.gpsimd.tensor_scalar(
-                    out=spread[:], in0=total_sq[:], scalar1=1.0 / D, scalar2=EPS, op0=ALU.mult, op1=ALU.add
+                    out=spread[:], in0=squares[i][:], scalar1=1.0 / D, scalar2=EPS, op0=ALU.mult, op1=ALU.add
                 )
                 mean_sq = tiny.tile([P, 2], F32, name="mean_sq")
                 nc.gpsimd.tensor_tensor(out=mean_sq[:], in0=mean[:], in1=mean[:], op=ALU.mult)
@@ -347,24 +364,28 @@ def tile_quantumcoherencelayer_kernel(
             def layer_norms(i):
                 mean, rstd = moments[i]
                 for part in range(2):
-                    normed = work2.tile([P, D], F32, name="normed", bufs=4)
-                    nc.vector.scalar_tensor_tensor(
-                        out=normed[:],
-                        in0=unit[i][:, part, :],
-                        scalar=mean[:, part : part + 1],
-                        in1=ln_w[:],
-                        op0=ALU.subtract,
-                        op1=ALU.mult,
+                    normed = work2.tile([P, BANKS, HALF], F32, name="normed", bufs=4)
+                    for b in range(BANKS):
+                        nc.vector.scalar_tensor_tensor(
+                            out=normed[:, b, :],
+                            in0=unit[i][:, part, HALF * b : HALF * (b + 1)],
+                            scalar=mean[:, part : part + 1],
+                            in1=affine[:, 0, b, :],
+                            op0=ALU.subtract,
+                            op1=ALU.mult,
+                        )
+                    for b in range(BANKS):
+                        nc.vector.scalar_tensor_tensor(
+                            out=normed[:, b, :],
+                            in0=normed[:, b, :],
+                            scalar=rstd[:, part : part + 1],
+                            in1=affine[:, 1, b, :],
+                            op0=ALU.mult,
+                            op1=ALU.add,
+                        )
+                    nc.sync.dma_start(
+                        out=out_rows[part][:, i, :], in_=normed[:].rearrange("p b n -> p (b n)")
                     )
-                    nc.vector.scalar_tensor_tensor(
-                        out=normed[:],
-                        in0=normed[:],
-                        scalar=rstd[:, part : part + 1],
-                        in1=ln_b[:],
-                        op0=ALU.mult,
-                        op1=ALU.add,
-                    )
-                    nc.sync.dma_start(out=out_rows[part][:, i, :], in_=normed[:])
 
             multiply(0)
             for step in range(TILES + LN_LAG):
@@ -374,9 +395,11 @@ def tile_quantumcoherencelayer_kernel(
                     reduce_angle(step)
                 if 0 <= step - 1 < TILES:
                     sine_and_cosine(step - 1)
+                if 0 <= step - 3 < TILES:
+                    row_moments(step - 3)
                 if 0 <= step - LN_LAG < TILES:
                     layer_norms(step - LN_LAG)
                 if 0 <= step - 1 < TILES:
                     rotate(step - 1)
                 if 0 <= step - 2 < TILES:
-                    row_moments(step - 2)
+                    sums_of_squares(step - 2)

@@ -20,6 +20,7 @@ ROWS = 2 * 1024
 TILES = ROWS // P
 HALF = 512
 BANKS = D // HALF
+CHUNKS = D // P
 K_PASSES = D // (4 * P)
 EPS = 1e-8
 ROUND_MAGIC = 12582912.0
@@ -65,9 +66,9 @@ def tile_quantumcoherencelayer_kernel(
         x_tiles = {}
         part1 = {}
 
-        with tc.tile_pool(name="x_in", bufs=3) as x_in, tc.tile_pool(
+        with tc.tile_pool(name="x_in", bufs=4) as x_in, tc.tile_pool(
             name="work1", bufs=2
-        ) as work1, tc.psum_pool(name="xt_psum", bufs=2) as xt_psum:
+        ) as work1, tc.psum_pool(name="psum1", bufs=2) as psum1:
 
             def load(i):
                 xri = x_in.tile([P, 2, D], BF16, name="xri")
@@ -135,9 +136,12 @@ def tile_quantumcoherencelayer_kernel(
                 shifted_sq = work1.tile([P, 2, D], F32, name="shifted_sq")
                 nc.scalar.activation(out=shifted_sq[:], in_=xri[:], func=ACT.Square, bias=eps[:])
                 plain_sq = work1.tile([P, 2, D], F32, name="plain_sq")
-                nc.scalar.activation(out=plain_sq[:], in_=xri[:], func=ACT.Square)
+                nc.scalar.activation(out=plain_sq[:, 0, :], in_=xri[:, 0, :], func=ACT.Square)
+                nc.gpsimd.tensor_tensor(
+                    out=plain_sq[:, 1, :], in0=xri[:, 1, :], in1=xri[:, 1, :], op=ALU.mult
+                )
                 words = xri[:, 0, :].bitcast(F32)
-                xt = xt_psum.tile([P, 2 * K_PASSES, P], F32, name="xt")
+                xt = psum1.tile([P, 2 * K_PASSES, P], F32, name="xt")
                 for g in range(K_PASSES):
                     for u in range(2):
                         nc.tensor.transpose(
@@ -145,24 +149,45 @@ def tile_quantumcoherencelayer_kernel(
                         )
                 grouped = work1.tile([P, K_PASSES, P, 2], F32, name="grouped", align_bytes=64)
                 nc.scalar.copy(out=grouped[:], in_=xt[:].rearrange("p (g u) r -> p g r u", u=2))
-                moduli = work1.tile([P, 2, D], F32, name="moduli")
+                norm_sq_t = psum1.tile([P, CHUNKS, P], F32, name="norm_sq_t")
+                for c in range(CHUNKS):
+                    for part in range(2):
+                        nc.tensor.matmul(
+                            out=norm_sq_t[:, c, :],
+                            lhsT=plain_sq[:, part, P * c : P * (c + 1)],
+                            rhs=ident[:],
+                            is_transpose=True,
+                            start=(part == 0),
+                            stop=(part == 1),
+                        )
+                inv_r = work1.tile([P, D], F32, name="inv_r")
                 nc.vector.tensor_tensor(
-                    out=moduli[:, 0, :], in0=shifted_sq[:, 0, :], in1=shifted_sq[:, 1, :], op=ALU.add
+                    out=inv_r[:], in0=shifted_sq[:, 0, :], in1=shifted_sq[:, 1, :], op=ALU.add
                 )
-                nc.vector.scalar_tensor_tensor(
-                    out=moduli[:, 1, :],
-                    in0=plain_sq[:, 0, :],
-                    scalar=EPS,
-                    in1=plain_sq[:, 1, :],
-                    op0=ALU.add,
-                    op1=ALU.add,
-                )
-                part1[i] = (grouped, moduli)
+                part1[i] = (grouped, inv_r, norm_sq_t)
 
             def coherence_and_unit(i):
                 xri = x_tiles[i]
-                grouped, moduli = part1[i]
-                nc.scalar.activation(out=moduli[:], in_=moduli[:], func=ACT.Abs_reciprocal_sqrt)
+                grouped, inv_r, norm_sq_t = part1[i]
+                nc.vector.quantize_mx(
+                    out=x_codes[i][:].bitcast(FP8X4),
+                    scales=x_scales[i][:],
+                    in_=grouped[:].rearrange("p g r u -> p (g r u)").bitcast(BF16),
+                )
+                nc.scalar.activation(out=inv_r[:], in_=inv_r[:], func=ACT.Abs_reciprocal_sqrt)
+                inv_n_t = work1.tile([P, CHUNKS, P], F32, name="inv_n_t")
+                per_bank = CHUNKS // BANKS
+                for b in range(BANKS):
+                    blocks = slice(per_bank * b, per_bank * (b + 1))
+                    nc.scalar.activation(
+                        out=inv_n_t[:, blocks, :],
+                        in_=norm_sq_t[:, blocks, :],
+                        func=ACT.Abs_reciprocal_sqrt,
+                        bias=eps[:],
+                    )
+                inv_n = psum1.tile([P, D], F32, name="inv_n", bufs=1)
+                for c in range(CHUNKS):
+                    nc.tensor.transpose(inv_n[:, P * c : P * (c + 1)], inv_n_t[:, c, :], ident[:])
                 sums = tiny.tile([P, 2], F32, name="sums")
                 for part in range(2):
                     unread = work1.tile([P, D], F32, name="unread")
@@ -170,22 +195,19 @@ def tile_quantumcoherencelayer_kernel(
                         out=unread[:],
                         in0=xri[:, part, :],
                         scalar=EPS,
-                        in1=moduli[:, 0, :],
+                        in1=inv_r[:],
                         op0=ALU.add,
                         op1=ALU.mult,
                         accum_out=sums[:, part : part + 1],
                     )
-                nc.vector.tensor_tensor(
-                    out=unit[i][:],
-                    in0=xri[:],
-                    in1=moduli[:, 1:2, :].to_broadcast([P, 2, D]),
-                    op=ALU.mult,
-                )
-                nc.vector.quantize_mx(
-                    out=x_codes[i][:].bitcast(FP8X4),
-                    scales=x_scales[i][:],
-                    in_=grouped[:].rearrange("p g r u -> p (g r u)").bitcast(BF16),
-                )
+                for b in range(BANKS):
+                    cols = slice(HALF * b, HALF * (b + 1))
+                    nc.vector.tensor_tensor(
+                        out=unit[i][:, :, cols],
+                        in0=xri[:, :, cols],
+                        in1=inv_n[:, cols].unsqueeze(1).to_broadcast([P, 2, HALF]),
+                        op=ALU.mult,
+                    )
                 sums_sq = tiny.tile([P, 2], F32, name="sums_sq")
                 nc.gpsimd.tensor_tensor(out=sums_sq[:], in0=sums[:], in1=sums[:], op=ALU.mult)
                 length_sq = tiny.tile([P, 1], F32, name="length_sq")

@@ -24,7 +24,8 @@ CHUNKS = D // P
 K_PASSES = D // (4 * P)
 EPS = 1e-8
 ROUND_MAGIC = 12582912.0
-LN_LAG = 4
+GAIN_BATCH = 8
+LN_LAG = 3
 
 FLOPS = 2 * ROWS * D * D
 
@@ -61,7 +62,8 @@ def tile_quantumcoherencelayer_kernel(
             keep.tile([P, K_PASSES * P], U8, name="x_scales%d" % i, align_bytes=64)
             for i in range(TILES)
         ]
-        turns_gain = [keep.tile([P, 1], F32, name="turns_gain%d" % i) for i in range(TILES)]
+        phase_sums = keep.tile([P, TILES, 2], F32, name="phase_sums")
+        turns_gain = keep.tile([P, TILES], F32, name="turns_gain")
 
         x_tiles = {}
         part1 = {}
@@ -97,6 +99,8 @@ def tile_quantumcoherencelayer_kernel(
             nc.vector.memset(minus_magic[:], -ROUND_MAGIC)
             minus_half = keep.tile([P, 2], F32, name="minus_half")
             nc.vector.memset(minus_half[:], -0.5)
+            warm_up = keep.tile([P, 1], F32, name="warm_up")
+            nc.scalar.activation(out=warm_up[:], in_=ones[:], func=ACT.Abs_reciprocal_sqrt)
 
             w_words = keep.tile([P, K_PASSES, 2 * D], U8, name="w_words", align_bytes=64)
             w_scales = keep.tile([P, K_PASSES, D], U8, name="w_scales", align_bytes=64)
@@ -188,7 +192,6 @@ def tile_quantumcoherencelayer_kernel(
                 inv_n = psum1.tile([P, D], F32, name="inv_n", bufs=1)
                 for c in range(CHUNKS):
                     nc.tensor.transpose(inv_n[:, P * c : P * (c + 1)], inv_n_t[:, c, :], ident[:])
-                sums = tiny.tile([P, 2], F32, name="sums")
                 for part in range(2):
                     unread = work1.tile([P, D], F32, name="unread")
                     nc.vector.scalar_tensor_tensor(
@@ -198,7 +201,7 @@ def tile_quantumcoherencelayer_kernel(
                         in1=inv_r[:],
                         op0=ALU.add,
                         op1=ALU.mult,
-                        accum_out=sums[:, part : part + 1],
+                        accum_out=phase_sums[:, i, part : part + 1],
                     )
                 for b in range(BANKS):
                     cols = slice(HALF * b, HALF * (b + 1))
@@ -208,14 +211,19 @@ def tile_quantumcoherencelayer_kernel(
                         in1=inv_n[:, cols].unsqueeze(1).to_broadcast([P, 2, HALF]),
                         op=ALU.mult,
                     )
-                sums_sq = tiny.tile([P, 2], F32, name="sums_sq")
-                nc.gpsimd.tensor_tensor(out=sums_sq[:], in0=sums[:], in1=sums[:], op=ALU.mult)
-                length_sq = tiny.tile([P, 1], F32, name="length_sq")
+
+            def coherence_gains(first):
+                batch = slice(first, first + GAIN_BATCH)
+                sums_sq = tiny.tile([P, GAIN_BATCH, 2], F32, name="sums_sq")
                 nc.gpsimd.tensor_tensor(
-                    out=length_sq[:], in0=sums_sq[:, 0:1], in1=sums_sq[:, 1:2], op=ALU.add
+                    out=sums_sq[:], in0=phase_sums[:, batch, :], in1=phase_sums[:, batch, :], op=ALU.mult
+                )
+                length_sq = tiny.tile([P, GAIN_BATCH], F32, name="length_sq")
+                nc.gpsimd.tensor_tensor(
+                    out=length_sq[:], in0=sums_sq[:, :, 0], in1=sums_sq[:, :, 1], op=ALU.add
                 )
                 nc.gpsimd.tensor_scalar(
-                    out=turns_gain[i][:],
+                    out=turns_gain[:, batch],
                     in0=length_sq[:],
                     scalar1=gain_slope[:],
                     scalar2=full_gain[:],
@@ -228,6 +236,8 @@ def tile_quantumcoherencelayer_kernel(
                     squares_and_words(step)
                 if step >= 1:
                     coherence_and_unit(step - 1)
+                if step >= 1 and step % GAIN_BATCH == 0:
+                    coherence_gains(step - GAIN_BATCH)
                 if step + 2 < TILES:
                     load(step + 2)
 
@@ -255,9 +265,10 @@ def tile_quantumcoherencelayer_kernel(
             products = {}
             angles = {}
             phasors = {}
+            factors = {}
             totals = {}
-            squares = {}
             moments = {}
+            scales = {}
 
             def multiply(i):
                 product = product_psum.tile([P, BANKS, HALF], F32, name="product")
@@ -282,7 +293,7 @@ def tile_quantumcoherencelayer_kernel(
                         out=whole_turns[:, b, :],
                         in_=product[:, b, :],
                         func=ACT.Identity,
-                        scale=turns_gain[i][:],
+                        scale=turns_gain[:, i : i + 1],
                         bias=magic[:],
                     )
                 nc.scalar.activation(
@@ -293,7 +304,7 @@ def tile_quantumcoherencelayer_kernel(
                     nc.vector.scalar_tensor_tensor(
                         out=frac[:, b, :],
                         in0=product[:, b, :],
-                        scalar=turns_gain[i][:],
+                        scalar=turns_gain[:, i : i + 1],
                         in1=whole_turns[:, b, :],
                         op0=ALU.mult,
                         op1=ALU.subtract,
@@ -319,25 +330,30 @@ def tile_quantumcoherencelayer_kernel(
                 )
                 phasors[i] = phasor
 
-            def rotate(i):
+            def phasor_products(i):
                 phasor = phasors[i]
-                by_sin = work2.tile([P, 2, D], F32, name="by_sin")
+                by_sin = work2.tile([P, 2, D], F32, name="by_sin", bufs=1)
                 nc.gpsimd.tensor_tensor(
                     out=by_sin[:],
                     in0=unit[i][:],
                     in1=phasor[:, 1:2, :].to_broadcast([P, 2, D]),
                     op=ALU.mult,
                 )
+                by_cos = work2.tile([P, 2, D], F32, name="by_cos", bufs=1)
                 nc.vector.tensor_tensor(
-                    out=unit[i][:],
+                    out=by_cos[:],
                     in0=unit[i][:],
                     in1=phasor[:, 0:1, :].to_broadcast([P, 2, D]),
                     op=ALU.mult,
                 )
+                factors[i] = (by_cos, by_sin)
+
+            def finish_rotation(i):
+                by_cos, by_sin = factors[i]
                 total = tiny.tile([P, 2], F32, name="total")
                 nc.vector.scalar_tensor_tensor(
                     out=unit[i][:, 0, :],
-                    in0=unit[i][:, 0, :],
+                    in0=by_cos[:, 0, :],
                     scalar=1.0,
                     in1=by_sin[:, 1, :],
                     op0=ALU.mult,
@@ -346,7 +362,7 @@ def tile_quantumcoherencelayer_kernel(
                 )
                 nc.vector.scalar_tensor_tensor(
                     out=unit[i][:, 1, :],
-                    in0=unit[i][:, 1, :],
+                    in0=by_cos[:, 1, :],
                     scalar=1.0,
                     in1=by_sin[:, 0, :],
                     op0=ALU.mult,
@@ -355,7 +371,7 @@ def tile_quantumcoherencelayer_kernel(
                 )
                 totals[i] = total
 
-            def sums_of_squares(i):
+            def row_moments(i):
                 total_sq = tiny.tile([P, 2], F32, name="total_sq")
                 for part in range(2):
                     unread = work2.tile([P, D], BF16, name="unread_sq")
@@ -365,26 +381,25 @@ def tile_quantumcoherencelayer_kernel(
                         func=ACT.Square,
                         accum_out=total_sq[:, part : part + 1],
                     )
-                squares[i] = total_sq
-
-            def row_moments(i):
                 mean = tiny.tile([P, 2], F32, name="mean")
-                nc.gpsimd.tensor_scalar(
-                    out=mean[:], in0=totals[i][:], scalar1=1.0 / D, scalar2=0.0, op0=ALU.mult, op1=ALU.add
-                )
-                spread = tiny.tile([P, 2], F32, name="spread")
-                nc.gpsimd.tensor_scalar(
-                    out=spread[:], in0=squares[i][:], scalar1=1.0 / D, scalar2=EPS, op0=ALU.mult, op1=ALU.add
-                )
+                nc.scalar.activation(out=mean[:], in_=totals[i][:], func=ACT.Copy, scale=1.0 / D)
                 mean_sq = tiny.tile([P, 2], F32, name="mean_sq")
-                nc.gpsimd.tensor_tensor(out=mean_sq[:], in0=mean[:], in1=mean[:], op=ALU.mult)
+                nc.scalar.activation(out=mean_sq[:], in_=totals[i][:], func=ACT.Square, scale=1.0 / D)
+                spread = tiny.tile([P, 2], F32, name="spread")
+                nc.scalar.activation(
+                    out=spread[:], in_=total_sq[:], func=ACT.Identity, scale=1.0 / D, bias=eps[:]
+                )
+                moments[i] = (mean, mean_sq, spread)
+
+            def inverse_deviation(i):
+                mean, mean_sq, spread = moments[i]
                 nc.gpsimd.tensor_tensor(out=spread[:], in0=spread[:], in1=mean_sq[:], op=ALU.subtract)
                 rstd = tiny.tile([P, 2], F32, name="rstd")
                 nc.gpsimd.tensor_tensor(out=rstd[:], in0=spread[:], in1=minus_half[:], op=ALU.pow)
-                moments[i] = (mean, rstd)
+                scales[i] = (mean, rstd)
 
             def layer_norms(i):
-                mean, rstd = moments[i]
+                mean, rstd = scales[i]
                 for part in range(2):
                     normed = work2.tile([P, BANKS, HALF], F32, name="normed", bufs=4)
                     for b in range(BANKS):
@@ -413,15 +428,17 @@ def tile_quantumcoherencelayer_kernel(
             for step in range(TILES + LN_LAG):
                 if step + 1 < TILES:
                     multiply(step + 1)
-                if step < TILES:
-                    reduce_angle(step)
                 if 0 <= step - 1 < TILES:
                     sine_and_cosine(step - 1)
-                if 0 <= step - 3 < TILES:
-                    row_moments(step - 3)
+                if 0 <= step - LN_LAG < TILES:
+                    inverse_deviation(step - LN_LAG)
+                if 0 <= step - 1 < TILES:
+                    phasor_products(step - 1)
+                if step < TILES:
+                    reduce_angle(step)
                 if 0 <= step - LN_LAG < TILES:
                     layer_norms(step - LN_LAG)
                 if 0 <= step - 1 < TILES:
-                    rotate(step - 1)
+                    finish_rotation(step - 1)
                 if 0 <= step - 2 < TILES:
-                    sums_of_squares(step - 2)
+                    row_moments(step - 2)

@@ -243,19 +243,20 @@ def tile_quantumcoherencelayer_kernel(
 
         with tc.tile_pool(name="work2", bufs=2, reuse_waits="tile") as work2, tc.psum_pool(
             name="affine_psum", bufs=1
-        ) as affine_psum, tc.psum_pool(name="product_psum", bufs=2) as product_psum:
+        ) as affine_psum, tc.psum_pool(name="product_psum", bufs=3) as product_psum:
+            nc.scalar.activation(out=warm_up[:], in_=ones[:], func=ACT.Sin)
             ln_rows = work2.tile([P, 2, D], BF16, name="ln_rows", bufs=1)
-            nc.vector.memset(ln_rows[:], 0.0)
+            nc.gpsimd.memset(ln_rows[:], 0.0)
             nc.sync.dma_start(out=ln_rows[0:1, 0, :], in_=ln_weight.rearrange("(o d) -> o d", o=1))
             nc.sync.dma_start(out=ln_rows[0:1, 1, :], in_=ln_bias.rearrange("(o d) -> o d", o=1))
             first_row = work2.tile([P, P], BF16, name="first_row", bufs=1)
-            nc.vector.memset(first_row[:], 0.0)
-            nc.vector.memset(first_row[0:1, :], 1.0)
-            affine = affine_psum.tile([P, 2, BANKS, HALF], F32, name="affine")
+            nc.gpsimd.memset(first_row[:], 0.0)
+            nc.gpsimd.memset(first_row[0:1, :], 1.0)
+            affine = affine_psum.tile([P, 2, D], BF16, name="affine")
             for which in range(2):
                 for b in range(BANKS):
                     nc.tensor.matmul(
-                        out=affine[:, which, b, :],
+                        out=affine[:, which, HALF * b : HALF * (b + 1)],
                         lhsT=first_row[:],
                         rhs=ln_rows[:, which, HALF * b : HALF * (b + 1)],
                         start=True,
@@ -400,29 +401,26 @@ def tile_quantumcoherencelayer_kernel(
 
             def layer_norms(i):
                 mean, rstd = scales[i]
+                normed = [work2.tile([P, D], F32, name="normed%d" % part) for part in range(2)]
                 for part in range(2):
-                    normed = work2.tile([P, BANKS, HALF], F32, name="normed", bufs=4)
-                    for b in range(BANKS):
-                        nc.vector.scalar_tensor_tensor(
-                            out=normed[:, b, :],
-                            in0=unit[i][:, part, HALF * b : HALF * (b + 1)],
-                            scalar=mean[:, part : part + 1],
-                            in1=affine[:, 0, b, :],
-                            op0=ALU.subtract,
-                            op1=ALU.mult,
-                        )
-                    for b in range(BANKS):
-                        nc.vector.scalar_tensor_tensor(
-                            out=normed[:, b, :],
-                            in0=normed[:, b, :],
-                            scalar=rstd[:, part : part + 1],
-                            in1=affine[:, 1, b, :],
-                            op0=ALU.mult,
-                            op1=ALU.add,
-                        )
-                    nc.sync.dma_start(
-                        out=out_rows[part][:, i, :], in_=normed[:].rearrange("p b n -> p (b n)")
+                    nc.vector.scalar_tensor_tensor(
+                        out=normed[part][:],
+                        in0=unit[i][:, part, :],
+                        scalar=mean[:, part : part + 1],
+                        in1=affine[:, 0, :],
+                        op0=ALU.subtract,
+                        op1=ALU.mult,
                     )
+                for part in range(2):
+                    nc.vector.scalar_tensor_tensor(
+                        out=normed[part][:],
+                        in0=normed[part][:],
+                        scalar=rstd[:, part : part + 1],
+                        in1=affine[:, 1, :],
+                        op0=ALU.mult,
+                        op1=ALU.add,
+                    )
+                    nc.sync.dma_start(out=out_rows[part][:, i, :], in_=normed[part][:])
 
             multiply(0)
             for step in range(TILES + LN_LAG):

@@ -242,8 +242,10 @@ def tile_quantumcoherencelayer_kernel(
                     load(step + 2)
 
         with tc.tile_pool(name="work2", bufs=2, reuse_waits="tile") as work2, tc.psum_pool(
-            name="affine_psum", bufs=1
-        ) as affine_psum, tc.psum_pool(name="product_psum", bufs=3) as product_psum:
+            name="affine_psum", bufs=1, reuse_waits="tile"
+        ) as affine_psum, tc.psum_pool(
+            name="product_psum", bufs=3, reuse_waits="tile"
+        ) as product_psum:
             nc.scalar.activation(out=warm_up[:], in_=ones[:], func=ACT.Sin)
             ln_rows = work2.tile([P, 2, D], BF16, name="ln_rows", bufs=1)
             nc.gpsimd.memset(ln_rows[:], 0.0)
@@ -253,15 +255,17 @@ def tile_quantumcoherencelayer_kernel(
             nc.gpsimd.memset(first_row[:], 0.0)
             nc.gpsimd.memset(first_row[0:1, :], 1.0)
             affine = affine_psum.tile([P, 2, D], BF16, name="affine")
-            for which in range(2):
-                for b in range(BANKS):
-                    nc.tensor.matmul(
-                        out=affine[:, which, HALF * b : HALF * (b + 1)],
-                        lhsT=first_row[:],
-                        rhs=ln_rows[:, which, HALF * b : HALF * (b + 1)],
-                        start=True,
-                        stop=True,
-                    )
+
+            def spread_affine():
+                for which in range(2):
+                    for b in range(BANKS):
+                        nc.tensor.matmul(
+                            out=affine[:, which, HALF * b : HALF * (b + 1)],
+                            lhsT=first_row[:],
+                            rhs=ln_rows[:, which, HALF * b : HALF * (b + 1)],
+                            start=True,
+                            stop=True,
+                        )
 
             products = {}
             angles = {}
@@ -426,6 +430,8 @@ def tile_quantumcoherencelayer_kernel(
             for step in range(TILES + LN_LAG):
                 if step + 1 < TILES:
                     multiply(step + 1)
+                if step == 0:
+                    spread_affine()
                 if 0 <= step - 1 < TILES:
                     sine_and_cosine(step - 1)
                 if 0 <= step - LN_LAG < TILES:

@@ -26,6 +26,7 @@ EPS = 1e-8
 ROUND_MAGIC = 12582912.0
 GAIN_BATCH = 8
 LN_LAG = 3
+GPSIMD_COS_FROM = 512
 
 FLOPS = 2 * ROWS * D * D
 
@@ -345,10 +346,19 @@ def tile_quantumcoherencelayer_kernel(
                     op=ALU.mult,
                 )
                 by_cos = work2.tile([P, 2, D], F32, name="by_cos", bufs=1)
+                nc.gpsimd.tensor_tensor(
+                    out=by_cos[:, 1, GPSIMD_COS_FROM:],
+                    in0=unit[i][:, 1, GPSIMD_COS_FROM:],
+                    in1=phasor[:, 0, GPSIMD_COS_FROM:],
+                    op=ALU.mult,
+                )
                 nc.vector.tensor_tensor(
-                    out=by_cos[:],
-                    in0=unit[i][:],
-                    in1=phasor[:, 0:1, :].to_broadcast([P, 2, D]),
+                    out=by_cos[:, 0, :], in0=unit[i][:, 0, :], in1=phasor[:, 0, :], op=ALU.mult
+                )
+                nc.vector.tensor_tensor(
+                    out=by_cos[:, 1, 0:GPSIMD_COS_FROM],
+                    in0=unit[i][:, 1, 0:GPSIMD_COS_FROM],
+                    in1=phasor[:, 0, 0:GPSIMD_COS_FROM],
                     op=ALU.mult,
                 )
                 factors[i] = (by_cos, by_sin)

@@ -400,15 +400,23 @@ def tile_quantumcoherencelayer_kernel(
                 nc.scalar.activation(out=mean[:], in_=totals[i][:], func=ACT.Copy, scale=1.0 / D)
                 mean_sq = tiny.tile([P, 2], F32, name="mean_sq")
                 nc.scalar.activation(out=mean_sq[:], in_=totals[i][:], func=ACT.Square, scale=1.0 / D)
-                spread = tiny.tile([P, 2], F32, name="spread")
+                shift = tiny.tile([P, 2], F32, name="shift")
                 nc.scalar.activation(
-                    out=spread[:], in_=total_sq[:], func=ACT.Identity, scale=1.0 / D, bias=eps[:]
+                    out=shift[:], in_=mean_sq[:], func=ACT.Identity, scale=-1.0, bias=eps[:]
                 )
-                moments[i] = (mean, mean_sq, spread)
+                spread = tiny.tile([P, 2], F32, name="spread")
+                for part in range(2):
+                    nc.scalar.activation(
+                        out=spread[:, part : part + 1],
+                        in_=total_sq[:, part : part + 1],
+                        func=ACT.Identity,
+                        scale=1.0 / D,
+                        bias=shift[:, part : part + 1],
+                    )
+                moments[i] = (mean, spread)
 
             def inverse_deviation(i):
-                mean, mean_sq, spread = moments[i]
-                nc.gpsimd.tensor_tensor(out=spread[:], in0=spread[:], in1=mean_sq[:], op=ALU.subtract)
+                mean, spread = moments[i]
                 rstd = tiny.tile([P, 2], F32, name="rstd")
                 nc.gpsimd.tensor_tensor(out=rstd[:], in0=spread[:], in1=minus_half[:], op=ALU.pow)
                 scales[i] = (mean, rstd)

@@ -21,12 +21,14 @@ TILES = ROWS // P
 HALF = 512
 BANKS = D // HALF
 CHUNKS = D // P
+PER_BANK = CHUNKS // BANKS
 K_PASSES = D // (4 * P)
 EPS = 1e-8
 ROUND_MAGIC = 12582912.0
+SUBS = 4
 GAIN_BATCH = 8
-LN_LAG = 3
-GPSIMD_COS_FROM = 512
+PLANES = 7
+SQUARE_SCALE = math.sqrt(1.0 / (2.0 * EPS))
 
 FLOPS = 2 * ROWS * D * D
 
@@ -54,7 +56,11 @@ def tile_quantumcoherencelayer_kernel(
         keep = whole.enter_context(tc.tile_pool(name="keep", bufs=1))
         tiny = whole.enter_context(tc.tile_pool(name="tiny", bufs=6))
 
-        unit = [keep.tile([P, 2, D], F32, name="unit%d" % i) for i in range(TILES)]
+        x_turned = [
+            keep.tile([P, 2, K_PASSES, P, 2], F32, name="x_turned%d" % i, align_bytes=64)
+            for i in range(TILES)
+        ]
+        inv_n = [keep.tile([P, D], F32, name="inv_n%d" % i) for i in range(TILES)]
         x_codes = [
             keep.tile([P, K_PASSES * P], U32, name="x_codes%d" % i, align_bytes=64)
             for i in range(TILES)
@@ -63,15 +69,27 @@ def tile_quantumcoherencelayer_kernel(
             keep.tile([P, K_PASSES * P], U8, name="x_scales%d" % i, align_bytes=64)
             for i in range(TILES)
         ]
-        phase_sums = keep.tile([P, TILES, 2], F32, name="phase_sums")
+        phase_sums = keep.tile([P, TILES, 2, BANKS], F32, name="phase_sums")
         turns_gain = keep.tile([P, TILES], F32, name="turns_gain")
 
-        x_tiles = {}
-        part1 = {}
+        psum = whole.enter_context(tc.psum_pool(name="psum", bufs=2))
+        affine = psum.tile([P, 2, D], BF16, name="affine", bufs=1)
+        turns = [keep.tile([P, SUBS, BANKS, P], F32, name="turns%d" % which) for which in range(2)]
+        products = {}
+        fractions = {}
 
-        with tc.tile_pool(name="x_in", bufs=4) as x_in, tc.tile_pool(
+        x_tiles = {}
+        words = {}
+        squares = {}
+        part_sums = {}
+        square_sums = {}
+        radii = {}
+        inv_r_turned = {}
+        inv_r = {}
+
+        with tc.tile_pool(name="x_in", bufs=5) as x_in, tc.tile_pool(
             name="work1", bufs=2
-        ) as work1, tc.psum_pool(name="psum1", bufs=2) as psum1:
+        ) as work1:
 
             def load(i):
                 xri = x_in.tile([P, 2, D], BF16, name="xri")
@@ -90,14 +108,16 @@ def tile_quantumcoherencelayer_kernel(
             nc.vector.tensor_scalar(
                 out=eps[:], in0=ones[:], scalar1=EPS, scalar2=None, op0=ALU.mult
             )
+            two_eps_sq = keep.tile([P, 1], F32, name="two_eps_sq")
+            nc.vector.tensor_scalar(
+                out=two_eps_sq[:], in0=ones[:], scalar1=2.0 * EPS * EPS, scalar2=None, op0=ALU.mult
+            )
             quarter_turn = keep.tile([P, 1], F32, name="quarter_turn")
             nc.vector.tensor_scalar(
                 out=quarter_turn[:], in0=ones[:], scalar1=math.pi / 2, scalar2=None, op0=ALU.mult
             )
             magic = keep.tile([P, 1], F32, name="magic")
             nc.vector.memset(magic[:], ROUND_MAGIC)
-            minus_magic = keep.tile([P, 1], F32, name="minus_magic")
-            nc.vector.memset(minus_magic[:], -ROUND_MAGIC)
             minus_half = keep.tile([P, 2], F32, name="minus_half")
             nc.vector.memset(minus_half[:], -0.5)
             warm_up = keep.tile([P, 1], F32, name="warm_up")
@@ -136,89 +156,138 @@ def tile_quantumcoherencelayer_kernel(
                 op0=ALU.mult,
             )
 
-            def squares_and_words(i):
-                xri = x_tiles[i]
-                shifted_sq = work1.tile([P, 2, D], F32, name="shifted_sq")
-                nc.scalar.activation(out=shifted_sq[:], in_=xri[:], func=ACT.Square, bias=eps[:])
-                plain_sq = work1.tile([P, 2, D], F32, name="plain_sq")
-                nc.scalar.activation(out=plain_sq[:, 0, :], in_=xri[:, 0, :], func=ACT.Square)
-                nc.gpsimd.tensor_tensor(
-                    out=plain_sq[:, 1, :], in0=xri[:, 1, :], in1=xri[:, 1, :], op=ALU.mult
-                )
-                words = xri[:, 0, :].bitcast(F32)
-                xt = psum1.tile([P, 2 * K_PASSES, P], F32, name="xt")
-                for g in range(K_PASSES):
-                    for u in range(2):
-                        nc.tensor.transpose(
-                            xt[:, 2 * g + u, :], words[:, 256 * g + u : 256 * (g + 1) : 2], ident[:]
-                        )
-                grouped = work1.tile([P, K_PASSES, P, 2], F32, name="grouped", align_bytes=64)
-                nc.scalar.copy(out=grouped[:], in_=xt[:].rearrange("p (g u) r -> p g r u", u=2))
-                norm_sq_t = psum1.tile([P, CHUNKS, P], F32, name="norm_sq_t")
-                for c in range(CHUNKS):
-                    for part in range(2):
+            ln_rows = work1.tile([P, 2, D], BF16, name="ln_rows", bufs=1)
+            nc.gpsimd.memset(ln_rows[:], 0.0)
+            nc.sync.dma_start(out=ln_rows[0:1, 0, :], in_=ln_weight.rearrange("(o d) -> o d", o=1))
+            nc.sync.dma_start(out=ln_rows[0:1, 1, :], in_=ln_bias.rearrange("(o d) -> o d", o=1))
+            first_row = work1.tile([P, P], BF16, name="first_row", bufs=1)
+            nc.gpsimd.memset(first_row[:], 0.0)
+            nc.gpsimd.memset(first_row[0:1, :], 1.0)
+            def spread_affine():
+                for which in range(2):
+                    for b in range(BANKS):
                         nc.tensor.matmul(
-                            out=norm_sq_t[:, c, :],
-                            lhsT=plain_sq[:, part, P * c : P * (c + 1)],
-                            rhs=ident[:],
-                            is_transpose=True,
-                            start=(part == 0),
-                            stop=(part == 1),
+                            out=affine[:, which, HALF * b : HALF * (b + 1)],
+                            lhsT=first_row[:],
+                            rhs=ln_rows[:, which, HALF * b : HALF * (b + 1)],
+                            start=True,
+                            stop=True,
                         )
-                inv_r = work1.tile([P, D], F32, name="inv_r")
-                nc.vector.tensor_tensor(
-                    out=inv_r[:], in0=shifted_sq[:, 0, :], in1=shifted_sq[:, 1, :], op=ALU.add
-                )
-                part1[i] = (grouped, inv_r, norm_sq_t)
 
-            def coherence_and_unit(i):
-                xri = x_tiles[i]
-                grouped, inv_r, norm_sq_t = part1[i]
+            def turn_words(i):
+                for part in range(2):
+                    x_words = x_tiles[i][:, part, :].bitcast(F32)
+                    xt = psum.tile([P, 2 * K_PASSES, P], F32, name="ring_a")
+                    for g in range(K_PASSES):
+                        for u in range(2):
+                            nc.tensor.transpose(
+                                xt[:, 2 * g + u, :], x_words[:, 256 * g + u : 256 * (g + 1) : 2], ident[:]
+                            )
+                    words[i, part] = xt
+
+            def keep_words(i):
+                for part in range(2):
+                    nc.vector.tensor_copy(
+                        out=x_turned[i][:, part],
+                        in_=words[i, part][:].rearrange("p (g u) r -> p g r u", u=2),
+                    )
+
+            def quantise(i):
                 nc.vector.quantize_mx(
                     out=x_codes[i][:].bitcast(FP8X4),
                     scales=x_scales[i][:],
-                    in_=grouped[:].rearrange("p g r u -> p (g r u)").bitcast(BF16),
+                    in_=x_turned[i][:, 0].rearrange("p g r u -> p (g r u)").bitcast(BF16),
                 )
-                nc.scalar.activation(out=inv_r[:], in_=inv_r[:], func=ACT.Abs_reciprocal_sqrt)
-                inv_n_t = work1.tile([P, CHUNKS, P], F32, name="inv_n_t")
-                per_bank = CHUNKS // BANKS
+
+            def square(i):
+                sq = work1.tile([P, 2, D], F32, name="sq")
+                nc.scalar.activation(
+                    out=sq[:], in_=x_tiles[i][:], func=ACT.Square, scale=SQUARE_SCALE
+                )
+                squares[i] = sq
+
+            def add_parts(i):
+                part_sum = work1.tile([P, D], F32, name="part_sum")
+                nc.gpsimd.tensor_tensor(
+                    out=part_sum[:], in0=x_tiles[i][:, 0, :], in1=x_tiles[i][:, 1, :], op=ALU.add
+                )
+                part_sums[i] = part_sum
+                square_sum = work1.tile([P, D], F32, name="square_sum")
+                nc.gpsimd.tensor_tensor(
+                    out=square_sum[:], in0=squares[i][:, 0, :], in1=squares[i][:, 1, :], op=ALU.add
+                )
+                square_sums[i] = square_sum
+
+            def root_n(i):
+                nc.scalar.activation(
+                    out=inv_n[i][:],
+                    in_=square_sums[i][:],
+                    func=ACT.Abs_reciprocal_sqrt,
+                    scale=2.0 * EPS,
+                    bias=eps[:],
+                )
+
+            def add_shift(i):
                 for b in range(BANKS):
-                    blocks = slice(per_bank * b, per_bank * (b + 1))
+                    radius = psum.tile([P, PER_BANK, P], F32, name="ring_b")
+                    for c in range(PER_BANK):
+                        cols = slice(P * (PER_BANK * b + c), P * (PER_BANK * b + c + 1))
+                        for which, addend in enumerate((square_sums[i], part_sums[i])):
+                            nc.tensor.matmul(
+                                out=radius[:, c, :],
+                                lhsT=addend[:, cols],
+                                rhs=ident[:],
+                                is_transpose=True,
+                                start=(which == 0),
+                                stop=(which == 1),
+                            )
+                    radii[i, b] = radius
+
+            def root_r(i):
+                turned = work1.tile([P, CHUNKS, P], F32, name="inv_r_turned")
+                for b in range(BANKS):
                     nc.scalar.activation(
-                        out=inv_n_t[:, blocks, :],
-                        in_=norm_sq_t[:, blocks, :],
+                        out=turned[:, PER_BANK * b : PER_BANK * (b + 1), :],
+                        in_=radii[i, b][:],
                         func=ACT.Abs_reciprocal_sqrt,
-                        bias=eps[:],
+                        scale=2.0 * EPS,
+                        bias=two_eps_sq[:],
                     )
-                inv_n = psum1.tile([P, D], F32, name="inv_n", bufs=1)
-                for c in range(CHUNKS):
-                    nc.tensor.transpose(inv_n[:, P * c : P * (c + 1)], inv_n_t[:, c, :], ident[:])
-                for part in range(2):
-                    unread = work1.tile([P, D], F32, name="unread")
-                    nc.vector.scalar_tensor_tensor(
-                        out=unread[:],
-                        in0=xri[:, part, :],
-                        scalar=EPS,
-                        in1=inv_r[:],
-                        op0=ALU.add,
-                        op1=ALU.mult,
-                        accum_out=phase_sums[:, i, part : part + 1],
-                    )
+                inv_r_turned[i] = turned
+
+            def turn_back(i):
                 for b in range(BANKS):
-                    cols = slice(HALF * b, HALF * (b + 1))
-                    nc.vector.tensor_tensor(
-                        out=unit[i][:, :, cols],
-                        in0=xri[:, :, cols],
-                        in1=inv_n[:, cols].unsqueeze(1).to_broadcast([P, 2, HALF]),
-                        op=ALU.mult,
-                    )
+                    rows = psum.tile([P, HALF], F32, name="ring_c")
+                    for c in range(PER_BANK):
+                        nc.tensor.transpose(
+                            rows[:, P * c : P * (c + 1)],
+                            inv_r_turned[i][:, PER_BANK * b + c, :],
+                            ident[:],
+                        )
+                    inv_r[i, b] = rows
+
+            def add_phases(i):
+                for b in range(BANKS):
+                    for part in range(2):
+                        unread = work1.tile([P, HALF], F32, name="unread")
+                        nc.vector.scalar_tensor_tensor(
+                            out=unread[:],
+                            in0=x_tiles[i][:, part, HALF * b : HALF * (b + 1)],
+                            scalar=EPS,
+                            in1=inv_r[i, b][:],
+                            op0=ALU.add,
+                            op1=ALU.mult,
+                            accum_out=phase_sums[:, i, part, b : b + 1],
+                        )
 
             def coherence_gains(first):
                 batch = slice(first, first + GAIN_BATCH)
-                sums_sq = tiny.tile([P, GAIN_BATCH, 2], F32, name="sums_sq")
+                sums = tiny.tile([P, GAIN_BATCH, 2], F32, name="sums")
                 nc.gpsimd.tensor_tensor(
-                    out=sums_sq[:], in0=phase_sums[:, batch, :], in1=phase_sums[:, batch, :], op=ALU.mult
+                    out=sums[:], in0=phase_sums[:, batch, :, 0], in1=phase_sums[:, batch, :, 1], op=ALU.add
                 )
+                sums_sq = tiny.tile([P, GAIN_BATCH, 2], F32, name="sums_sq")
+                nc.gpsimd.tensor_tensor(out=sums_sq[:], in0=sums[:], in1=sums[:], op=ALU.mult)
                 length_sq = tiny.tile([P, GAIN_BATCH], F32, name="length_sq")
                 nc.gpsimd.tensor_tensor(
                     out=length_sq[:], in0=sums_sq[:, :, 0], in1=sums_sq[:, :, 1], op=ALU.add
@@ -232,56 +301,12 @@ def tile_quantumcoherencelayer_kernel(
                     op1=ALU.add,
                 )
 
-            for step in range(TILES + 1):
-                if step < TILES:
-                    squares_and_words(step)
-                if step >= 1:
-                    coherence_and_unit(step - 1)
-                if step >= 1 and step % GAIN_BATCH == 0:
-                    coherence_gains(step - GAIN_BATCH)
-                if step + 2 < TILES:
-                    load(step + 2)
-
-        with tc.tile_pool(name="work2", bufs=2, reuse_waits="tile") as work2, tc.psum_pool(
-            name="affine_psum", bufs=1, reuse_waits="tile"
-        ) as affine_psum, tc.psum_pool(
-            name="product_psum", bufs=3, reuse_waits="tile"
-        ) as product_psum:
-            nc.scalar.activation(out=warm_up[:], in_=ones[:], func=ACT.Sin)
-            ln_rows = work2.tile([P, 2, D], BF16, name="ln_rows", bufs=1)
-            nc.gpsimd.memset(ln_rows[:], 0.0)
-            nc.sync.dma_start(out=ln_rows[0:1, 0, :], in_=ln_weight.rearrange("(o d) -> o d", o=1))
-            nc.sync.dma_start(out=ln_rows[0:1, 1, :], in_=ln_bias.rearrange("(o d) -> o d", o=1))
-            first_row = work2.tile([P, P], BF16, name="first_row", bufs=1)
-            nc.gpsimd.memset(first_row[:], 0.0)
-            nc.gpsimd.memset(first_row[0:1, :], 1.0)
-            affine = affine_psum.tile([P, 2, D], BF16, name="affine")
-
-            def spread_affine():
-                for which in range(2):
-                    for b in range(BANKS):
-                        nc.tensor.matmul(
-                            out=affine[:, which, HALF * b : HALF * (b + 1)],
-                            lhsT=first_row[:],
-                            rhs=ln_rows[:, which, HALF * b : HALF * (b + 1)],
-                            start=True,
-                            stop=True,
-                        )
-
-            products = {}
-            angles = {}
-            phasors = {}
-            factors = {}
-            totals = {}
-            moments = {}
-            scales = {}
-
             def multiply(i):
-                product = product_psum.tile([P, BANKS, HALF], F32, name="product")
                 for b in range(BANKS):
+                    product = psum.tile([P, HALF], F32, name="ring_a")
                     for g in range(K_PASSES):
                         nc.tensor.matmul_mx(
-                            out=product[:, b, :],
+                            out=product[:],
                             lhsT=x_codes[i][:, P * g : P * (g + 1)].bitcast(FP8X4),
                             lhsT_scale=x_scales[i][:, P * g : P * (g + 1)],
                             rhs=w_words[:, g, 2 * HALF * b : 2 * HALF * (b + 1)].bitcast(FP4X4),
@@ -289,117 +314,197 @@ def tile_quantumcoherencelayer_kernel(
                             start=(g == 0),
                             stop=(g == K_PASSES - 1),
                         )
-                products[i] = product
+                    products[i, b] = product
 
-            def reduce_angle(i):
-                product = products[i]
-                whole_turns = work2.tile([P, BANKS, HALF], F32, name="whole_turns")
+            def count_turns(i):
+                angle, whole = turns
                 for b in range(BANKS):
+                    by_sub = products[i, b][:].rearrange("p (q t) -> p t q", t=SUBS)
                     nc.scalar.activation(
-                        out=whole_turns[:, b, :],
-                        in_=product[:, b, :],
+                        out=angle[:, :, b, :], in_=by_sub, func=ACT.Copy, scale=turns_gain[:, i : i + 1]
+                    )
+                    nc.scalar.activation(
+                        out=whole[:, :, b, :],
+                        in_=by_sub,
                         func=ACT.Identity,
                         scale=turns_gain[:, i : i + 1],
                         bias=magic[:],
                     )
-                nc.scalar.activation(
-                    out=whole_turns[:], in_=whole_turns[:], func=ACT.Identity, bias=minus_magic[:]
+
+            def negate_whole(i):
+                whole = turns[1]
+                nc.gpsimd.tensor_scalar(
+                    out=whole[:],
+                    in0=whole[:],
+                    scalar1=-1.0,
+                    scalar2=ROUND_MAGIC,
+                    op0=ALU.mult,
+                    op1=ALU.add,
                 )
-                frac = work2.tile([P, BANKS, HALF], F32, name="frac")
+
+            def fraction(i):
                 for b in range(BANKS):
-                    nc.vector.scalar_tensor_tensor(
-                        out=frac[:, b, :],
-                        in0=product[:, b, :],
-                        scalar=turns_gain[:, i : i + 1],
-                        in1=whole_turns[:, b, :],
-                        op0=ALU.mult,
-                        op1=ALU.subtract,
-                    )
-                angles[i] = (frac, whole_turns)
+                    frac = psum.tile([P, SUBS, P], F32, name="ring_b")
+                    for t in range(SUBS):
+                        for which in range(2):
+                            nc.tensor.matmul(
+                                out=frac[:, t, :],
+                                lhsT=turns[which][:, t, b, :],
+                                rhs=ident[:],
+                                is_transpose=True,
+                                start=(which == 0),
+                                stop=(which == 1),
+                            )
+                    fractions[i, b] = frac
+
+            for step in range(TILES + 2):
+                if 0 <= step - 1 < TILES:
+                    add_shift(step - 1)
+                if 0 <= step - 2:
+                    turn_back(step - 2)
+                if step < TILES:
+                    turn_words(step)
+                    square(step)
+                    add_parts(step)
+                if 0 <= step - 1 < TILES:
+                    root_n(step - 1)
+                    root_r(step - 1)
+                    quantise(step - 1)
+                if 0 <= step - 2:
+                    add_phases(step - 2)
+                if step < TILES:
+                    keep_words(step)
+                if step == GAIN_BATCH + 1:
+                    coherence_gains(0)
+                if step == TILES:
+                    multiply(0)
+                    count_turns(0)
+                    negate_whole(0)
+                    nc.scalar.activation(out=warm_up[:], in_=ones[:], func=ACT.Sin)
+                if step == TILES + 1:
+                    fraction(0)
+                    coherence_gains(GAIN_BATCH)
+                    multiply(1)
+                if step + 2 < TILES:
+                    load(step + 2)
+                if step == 1:
+                    spread_affine()
+
+        with tc.tile_pool(name="work2", bufs=2, reuse_waits="tile") as work2:
+            phasors = {}
+            planes = {}
+            rotated = {}
+            units = {}
+            totals = {}
+            moments = {}
+            scales = {}
 
             def sine_and_cosine(i):
-                frac, abs_frac = angles[i]
-                nc.scalar.activation(out=abs_frac[:], in_=frac[:], func=ACT.Abs)
-                phasor = work2.tile([P, 2, D], F32, name="phasor")
+                phasor = work2.tile([P, 2, SUBS, BANKS, P], F32, name="phasor")
+                for b in range(BANKS):
+                    nc.scalar.activation(out=phasor[:, 0, :, b, :], in_=fractions[i, b][:], func=ACT.Abs)
+                    nc.scalar.activation(
+                        out=phasor[:, 1, :, b, :], in_=fractions[i, b][:], func=ACT.Sin, scale=2.0 * math.pi
+                    )
                 nc.scalar.activation(
-                    out=phasor[:, 1, :],
-                    in_=frac[:].rearrange("p b n -> p (b n)"),
-                    func=ACT.Sin,
-                    scale=2.0 * math.pi,
-                )
-                nc.scalar.activation(
-                    out=phasor[:, 0, :],
-                    in_=abs_frac[:].rearrange("p b n -> p (b n)"),
+                    out=phasor[:, 0],
+                    in_=phasor[:, 0],
                     func=ACT.Sin,
                     scale=-2.0 * math.pi,
                     bias=quarter_turn[:],
                 )
                 phasors[i] = phasor
 
-            def phasor_products(i):
-                phasor = phasors[i]
-                by_sin = work2.tile([P, 2, D], F32, name="by_sin", bufs=1)
-                nc.gpsimd.tensor_tensor(
-                    out=by_sin[:],
-                    in0=unit[i][:],
-                    in1=phasor[:, 1:2, :].to_broadcast([P, 2, D]),
-                    op=ALU.mult,
+            def turned_part(i, part):
+                return (
+                    x_turned[i][:, part]
+                    .rearrange("p g r u -> p (g r u)")
+                    .bitcast(BF16)
+                    .rearrange("p (g r t) -> p t g r", g=K_PASSES, t=SUBS)
                 )
-                by_cos = work2.tile([P, 2, D], F32, name="by_cos", bufs=1)
-                nc.gpsimd.tensor_tensor(
-                    out=by_cos[:, 1, GPSIMD_COS_FROM:],
-                    in0=unit[i][:, 1, GPSIMD_COS_FROM:],
-                    in1=phasor[:, 0, GPSIMD_COS_FROM:],
-                    op=ALU.mult,
-                )
-                nc.vector.tensor_tensor(
-                    out=by_cos[:, 0, :], in0=unit[i][:, 0, :], in1=phasor[:, 0, :], op=ALU.mult
-                )
-                nc.vector.tensor_tensor(
-                    out=by_cos[:, 1, 0:GPSIMD_COS_FROM],
-                    in0=unit[i][:, 1, 0:GPSIMD_COS_FROM],
-                    in1=phasor[:, 0, 0:GPSIMD_COS_FROM],
-                    op=ALU.mult,
-                )
-                factors[i] = (by_cos, by_sin)
 
-            def finish_rotation(i):
-                by_cos, by_sin = factors[i]
-                total = tiny.tile([P, 2], F32, name="total")
-                nc.vector.scalar_tensor_tensor(
-                    out=unit[i][:, 0, :],
-                    in0=by_cos[:, 0, :],
-                    scalar=1.0,
-                    in1=by_sin[:, 1, :],
-                    op0=ALU.mult,
-                    op1=ALU.subtract,
-                    accum_out=total[:, 0:1],
+            def open_planes(i):
+                planes[i] = [
+                    work2.tile([P, SUBS, BANKS, P], F32, name="plane", bufs=PLANES) for which in range(4)
+                ]
+                rotated[i] = ((planes[i][0], planes[i][3]), (planes[i][1], planes[i][2]))
+
+            def product_of_gpsimd(i, which, banks):
+                nc.gpsimd.tensor_tensor(
+                    out=planes[i][which][:, :, banks, :],
+                    in0=turned_part(i, which // 2)[:, :, banks, :],
+                    in1=phasors[i][:, which % 2, :, banks, :],
+                    op=ALU.mult,
                 )
+
+            def product_of_vector(i, which, banks):
                 nc.vector.scalar_tensor_tensor(
-                    out=unit[i][:, 1, :],
-                    in0=by_cos[:, 1, :],
-                    scalar=1.0,
-                    in1=by_sin[:, 0, :],
+                    out=planes[i][which][:, :, banks, :],
+                    in0=turned_part(i, which // 2)[:, :, banks, :],
+                    scalar=-1.0 if which == 3 else 1.0,
+                    in1=phasors[i][:, which % 2, :, banks, :],
                     op0=ALU.mult,
-                    op1=ALU.add,
-                    accum_out=total[:, 1:2],
+                    op1=ALU.mult,
                 )
-                totals[i] = total
+
+            def add_products(i, part, b):
+                rows = psum.tile([P, SUBS, P], F32, name="ring_c")
+                for t in range(SUBS):
+                    for which in range(2):
+                        nc.tensor.matmul(
+                            out=rows[:, t, :],
+                            lhsT=rotated[i][part][which][:, t, b, :],
+                            rhs=ident[:],
+                            is_transpose=True,
+                            start=(which == 0),
+                            stop=(which == 1),
+                        )
+                return rows
+
+            def normalise(i, part, b, rows):
+                nc.vector.scalar_tensor_tensor(
+                    out=units[i][:, part, HALF * b : HALF * (b + 1)].rearrange(
+                        "p (q t) -> p q t", t=SUBS
+                    ),
+                    in0=rows[:].rearrange("p t q -> p q t"),
+                    scalar=1.0,
+                    in1=inv_n[i][:, HALF * b : HALF * (b + 1)].rearrange("p (q t) -> p q t", t=SUBS),
+                    op0=ALU.mult,
+                    op1=ALU.mult,
+                    accum_out=totals[i][:, part, b : b + 1],
+                )
+
+            def rotate(i, part):
+                if part == 0:
+                    units[i] = work2.tile([P, 2, D], F32, name="unit", bufs=3)
+                    totals[i] = tiny.tile([P, 2, BANKS], F32, name="total")
+                for b in range(BANKS):
+                    normalise(i, part, b, add_products(i, part, b))
+
+            row_totals = {}
+
+            def join_totals(i):
+                row_total = tiny.tile([P, 2], F32, name="row_total")
+                nc.vector.tensor_tensor(
+                    out=row_total[:], in0=totals[i][:, :, 0], in1=totals[i][:, :, 1], op=ALU.add
+                )
+                row_totals[i] = row_total
 
             def row_moments(i):
+                total = row_totals[i]
                 total_sq = tiny.tile([P, 2], F32, name="total_sq")
                 for part in range(2):
-                    unread = work2.tile([P, D], BF16, name="unread_sq")
+                    unread = work2.tile([P, D], BF16, name="unread_sq", bufs=1)
                     nc.scalar.activation(
                         out=unread[:],
-                        in_=unit[i][:, part, :],
+                        in_=units[i][:, part, :],
                         func=ACT.Square,
                         accum_out=total_sq[:, part : part + 1],
                     )
                 mean = tiny.tile([P, 2], F32, name="mean")
-                nc.scalar.activation(out=mean[:], in_=totals[i][:], func=ACT.Copy, scale=1.0 / D)
+                nc.scalar.activation(out=mean[:], in_=total[:], func=ACT.Copy, scale=1.0 / D)
                 mean_sq = tiny.tile([P, 2], F32, name="mean_sq")
-                nc.scalar.activation(out=mean_sq[:], in_=totals[i][:], func=ACT.Square, scale=1.0 / D)
+                nc.scalar.activation(out=mean_sq[:], in_=total[:], func=ACT.Square, scale=1.0 / D)
                 shift = tiny.tile([P, 2], F32, name="shift")
                 nc.scalar.activation(
                     out=shift[:], in_=mean_sq[:], func=ACT.Identity, scale=-1.0, bias=eps[:]
@@ -423,11 +528,10 @@ def tile_quantumcoherencelayer_kernel(
 
             def layer_norms(i):
                 mean, rstd = scales[i]
-                normed = [work2.tile([P, D], F32, name="normed%d" % part) for part in range(2)]
                 for part in range(2):
                     nc.vector.scalar_tensor_tensor(
-                        out=normed[part][:],
-                        in0=unit[i][:, part, :],
+                        out=units[i][:, part, :],
+                        in0=units[i][:, part, :],
                         scalar=mean[:, part : part + 1],
                         in1=affine[:, 0, :],
                         op0=ALU.subtract,
@@ -435,32 +539,50 @@ def tile_quantumcoherencelayer_kernel(
                     )
                 for part in range(2):
                     nc.vector.scalar_tensor_tensor(
-                        out=normed[part][:],
-                        in0=normed[part][:],
+                        out=units[i][:, part, :],
+                        in0=units[i][:, part, :],
                         scalar=rstd[:, part : part + 1],
                         in1=affine[:, 1, :],
                         op0=ALU.mult,
                         op1=ALU.add,
                     )
-                    nc.sync.dma_start(out=out_rows[part][:, i, :], in_=normed[part][:])
+                    nc.sync.dma_start(out=out_rows[part][:, i, :], in_=units[i][:, part, :])
 
-            multiply(0)
-            for step in range(TILES + LN_LAG):
-                if step + 1 < TILES:
-                    multiply(step + 1)
-                if step == 0:
-                    spread_affine()
-                if 0 <= step - 1 < TILES:
-                    sine_and_cosine(step - 1)
-                if 0 <= step - LN_LAG < TILES:
-                    inverse_deviation(step - LN_LAG)
-                if 0 <= step - 1 < TILES:
-                    phasor_products(step - 1)
-                if step < TILES:
-                    reduce_angle(step)
-                if 0 <= step - LN_LAG < TILES:
-                    layer_norms(step - LN_LAG)
-                if 0 <= step - 1 < TILES:
-                    finish_rotation(step - 1)
+            sine_and_cosine(0)
+            count_turns(1)
+            negate_whole(1)
+            for step in range(0, TILES + 2):
+                if 0 <= step < TILES:
+                    open_planes(step)
+                if 0 <= step < TILES:
+                    product_of_gpsimd(step, 0, slice(0, BANKS))
                 if 0 <= step - 2 < TILES:
                     row_moments(step - 2)
+                if 0 <= step - 2 < TILES:
+                    inverse_deviation(step - 2)
+                if 0 <= step < TILES:
+                    product_of_gpsimd(step, 1, slice(0, BANKS))
+                if 0 <= step < TILES:
+                    product_of_gpsimd(step, 2, slice(0, 1))
+                if 0 <= step - 1 < TILES:
+                    rotate(step - 1, 0)
+                if 0 <= step + 1 < TILES:
+                    fraction(step + 1)
+                if 0 <= step < TILES:
+                    product_of_vector(step, 3, slice(0, BANKS))
+                if 0 <= step < TILES:
+                    product_of_vector(step, 2, slice(1, 2))
+                if 0 <= step - 1 < TILES:
+                    rotate(step - 1, 1)
+                if 0 <= step - 1 < TILES:
+                    join_totals(step - 1)
+                if 0 <= step + 1 < TILES:
+                    sine_and_cosine(step + 1)
+                if 0 <= step + 2 < TILES:
+                    multiply(step + 2)
+                if 0 <= step + 2 < TILES:
+                    count_turns(step + 2)
+                if 0 <= step + 2 < TILES:
+                    negate_whole(step + 2)
+                if 0 <= step - 2 < TILES:
+                    layer_norms(step - 2)

@@ -27,7 +27,7 @@ EPS = 1e-8
 ROUND_MAGIC = 12582912.0
 SUBS = 4
 GAIN_BATCH = 8
-PLANES = 7
+PLANES = 6
 SQUARE_SCALE = math.sqrt(1.0 / (2.0 * EPS))
 
 FLOPS = 2 * ROWS * D * D
@@ -54,7 +54,7 @@ def tile_quantumcoherencelayer_kernel(
 
     with tc.manual_schedule(), ExitStack() as whole:
         keep = whole.enter_context(tc.tile_pool(name="keep", bufs=1))
-        tiny = whole.enter_context(tc.tile_pool(name="tiny", bufs=6))
+        tiny = whole.enter_context(tc.tile_pool(name="tiny", bufs=3))
 
         x_turned = [
             keep.tile([P, 2, K_PASSES, P, 2], F32, name="x_turned%d" % i, align_bytes=64)
@@ -74,7 +74,10 @@ def tile_quantumcoherencelayer_kernel(
 
         psum = whole.enter_context(tc.psum_pool(name="psum", bufs=2))
         affine = psum.tile([P, 2, D], BF16, name="affine", bufs=1)
-        turns = [keep.tile([P, SUBS, BANKS, P], F32, name="turns%d" % which) for which in range(2)]
+        turns = [
+            [keep.tile([P, SUBS, BANKS, P], F32, name="turns%d%d" % (turn, which)) for which in range(2)]
+            for turn in range(2)
+        ]
         products = {}
         fractions = {}
 
@@ -87,7 +90,7 @@ def tile_quantumcoherencelayer_kernel(
         inv_r_turned = {}
         inv_r = {}
 
-        with tc.tile_pool(name="x_in", bufs=5) as x_in, tc.tile_pool(
+        with tc.tile_pool(name="x_in", bufs=4) as x_in, tc.tile_pool(
             name="work1", bufs=2
         ) as work1:
 
@@ -282,13 +285,13 @@ def tile_quantumcoherencelayer_kernel(
 
             def coherence_gains(first):
                 batch = slice(first, first + GAIN_BATCH)
-                sums = tiny.tile([P, GAIN_BATCH, 2], F32, name="sums")
+                sums = tiny.tile([P, GAIN_BATCH, 2], F32, name="sums", bufs=1)
                 nc.gpsimd.tensor_tensor(
                     out=sums[:], in0=phase_sums[:, batch, :, 0], in1=phase_sums[:, batch, :, 1], op=ALU.add
                 )
-                sums_sq = tiny.tile([P, GAIN_BATCH, 2], F32, name="sums_sq")
+                sums_sq = tiny.tile([P, GAIN_BATCH, 2], F32, name="sums_sq", bufs=1)
                 nc.gpsimd.tensor_tensor(out=sums_sq[:], in0=sums[:], in1=sums[:], op=ALU.mult)
-                length_sq = tiny.tile([P, GAIN_BATCH], F32, name="length_sq")
+                length_sq = tiny.tile([P, GAIN_BATCH], F32, name="length_sq", bufs=1)
                 nc.gpsimd.tensor_tensor(
                     out=length_sq[:], in0=sums_sq[:, :, 0], in1=sums_sq[:, :, 1], op=ALU.add
                 )
@@ -317,7 +320,7 @@ def tile_quantumcoherencelayer_kernel(
                     products[i, b] = product
 
             def count_turns(i):
-                angle, whole = turns
+                angle, whole = turns[i % 2]
                 for b in range(BANKS):
                     by_sub = products[i, b][:].rearrange("p (q t) -> p t q", t=SUBS)
                     nc.scalar.activation(
@@ -332,8 +335,8 @@ def tile_quantumcoherencelayer_kernel(
                     )
 
             def negate_whole(i):
-                whole = turns[1]
-                nc.gpsimd.tensor_scalar(
+                whole = turns[i % 2][1]
+                nc.vector.tensor_scalar(
                     out=whole[:],
                     in0=whole[:],
                     scalar1=-1.0,
@@ -349,7 +352,7 @@ def tile_quantumcoherencelayer_kernel(
                         for which in range(2):
                             nc.tensor.matmul(
                                 out=frac[:, t, :],
-                                lhsT=turns[which][:, t, b, :],
+                                lhsT=turns[i % 2][which][:, t, b, :],
                                 rhs=ident[:],
                                 is_transpose=True,
                                 start=(which == 0),
@@ -394,6 +397,7 @@ def tile_quantumcoherencelayer_kernel(
             phasors = {}
             planes = {}
             rotated = {}
+            rotated_rows = {}
             units = {}
             totals = {}
             moments = {}
@@ -424,14 +428,13 @@ def tile_quantumcoherencelayer_kernel(
                 )
 
             def open_planes(i):
-                planes[i] = [
-                    work2.tile([P, SUBS, BANKS, P], F32, name="plane", bufs=PLANES) for which in range(4)
-                ]
-                rotated[i] = ((planes[i][0], planes[i][3]), (planes[i][1], planes[i][2]))
+                for which in (3, 0, 1, 2):
+                    planes[i, which] = work2.tile([P, SUBS, BANKS, P], F32, name="plane", bufs=PLANES)
+                rotated[i] = ((planes[i, 0], planes[i, 3]), (planes[i, 1], planes[i, 2]))
 
             def product_of_gpsimd(i, which, banks):
                 nc.gpsimd.tensor_tensor(
-                    out=planes[i][which][:, :, banks, :],
+                    out=planes[i, which][:, :, banks, :],
                     in0=turned_part(i, which // 2)[:, :, banks, :],
                     in1=phasors[i][:, which % 2, :, banks, :],
                     op=ALU.mult,
@@ -439,13 +442,16 @@ def tile_quantumcoherencelayer_kernel(
 
             def product_of_vector(i, which, banks):
                 nc.vector.scalar_tensor_tensor(
-                    out=planes[i][which][:, :, banks, :],
+                    out=planes[i, which][:, :, banks, :],
                     in0=turned_part(i, which // 2)[:, :, banks, :],
                     scalar=-1.0 if which == 3 else 1.0,
                     in1=phasors[i][:, which % 2, :, banks, :],
                     op0=ALU.mult,
                     op1=ALU.mult,
                 )
+
+            def hold_gpsimd(i):
+                nc.vector.memset(planes[i, 0][:, 0, 0, 0:1], 0.0)
 
             def add_products(i, part, b):
                 rows = psum.tile([P, SUBS, P], F32, name="ring_c")
@@ -459,27 +465,23 @@ def tile_quantumcoherencelayer_kernel(
                             start=(which == 0),
                             stop=(which == 1),
                         )
-                return rows
+                rotated_rows[i, part, b] = rows
 
-            def normalise(i, part, b, rows):
+            def normalise(i, part, b):
+                if (part, b) == (0, 0):
+                    units[i] = work2.tile([P, 2, D], F32, name="unit", bufs=3)
+                    totals[i] = tiny.tile([P, 2, BANKS], F32, name="total")
                 nc.vector.scalar_tensor_tensor(
                     out=units[i][:, part, HALF * b : HALF * (b + 1)].rearrange(
                         "p (q t) -> p q t", t=SUBS
                     ),
-                    in0=rows[:].rearrange("p t q -> p q t"),
+                    in0=rotated_rows[i, part, b][:].rearrange("p t q -> p q t"),
                     scalar=1.0,
                     in1=inv_n[i][:, HALF * b : HALF * (b + 1)].rearrange("p (q t) -> p q t", t=SUBS),
                     op0=ALU.mult,
                     op1=ALU.mult,
                     accum_out=totals[i][:, part, b : b + 1],
                 )
-
-            def rotate(i, part):
-                if part == 0:
-                    units[i] = work2.tile([P, 2, D], F32, name="unit", bufs=3)
-                    totals[i] = tiny.tile([P, 2, BANKS], F32, name="total")
-                for b in range(BANKS):
-                    normalise(i, part, b, add_products(i, part, b))
 
             row_totals = {}
 
@@ -492,6 +494,8 @@ def tile_quantumcoherencelayer_kernel(
 
             def row_moments(i):
                 total = row_totals[i]
+                mean = tiny.tile([P, 2], F32, name="mean")
+                nc.scalar.activation(out=mean[:], in_=total[:], func=ACT.Copy, scale=1.0 / D)
                 total_sq = tiny.tile([P, 2], F32, name="total_sq")
                 for part in range(2):
                     unread = work2.tile([P, D], BF16, name="unread_sq", bufs=1)
@@ -501,8 +505,6 @@ def tile_quantumcoherencelayer_kernel(
                         func=ACT.Square,
                         accum_out=total_sq[:, part : part + 1],
                     )
-                mean = tiny.tile([P, 2], F32, name="mean")
-                nc.scalar.activation(out=mean[:], in_=total[:], func=ACT.Copy, scale=1.0 / D)
                 mean_sq = tiny.tile([P, 2], F32, name="mean_sq")
                 nc.scalar.activation(out=mean_sq[:], in_=total[:], func=ACT.Square, scale=1.0 / D)
                 shift = tiny.tile([P, 2], F32, name="shift")
@@ -526,63 +528,71 @@ def tile_quantumcoherencelayer_kernel(
                 nc.gpsimd.tensor_tensor(out=rstd[:], in0=spread[:], in1=minus_half[:], op=ALU.pow)
                 scales[i] = (mean, rstd)
 
-            def layer_norms(i):
-                mean, rstd = scales[i]
-                for part in range(2):
-                    nc.vector.scalar_tensor_tensor(
-                        out=units[i][:, part, :],
-                        in0=units[i][:, part, :],
-                        scalar=mean[:, part : part + 1],
-                        in1=affine[:, 0, :],
-                        op0=ALU.subtract,
-                        op1=ALU.mult,
-                    )
-                for part in range(2):
-                    nc.vector.scalar_tensor_tensor(
-                        out=units[i][:, part, :],
-                        in0=units[i][:, part, :],
-                        scalar=rstd[:, part : part + 1],
-                        in1=affine[:, 1, :],
-                        op0=ALU.mult,
-                        op1=ALU.add,
-                    )
-                    nc.sync.dma_start(out=out_rows[part][:, i, :], in_=units[i][:, part, :])
+            def norm_first(i, part):
+                nc.vector.scalar_tensor_tensor(
+                    out=units[i][:, part, :],
+                    in0=units[i][:, part, :],
+                    scalar=moments[i][0][:, part : part + 1],
+                    in1=affine[:, 0, :],
+                    op0=ALU.subtract,
+                    op1=ALU.mult,
+                )
+
+            def norm_second(i, part):
+                nc.vector.scalar_tensor_tensor(
+                    out=units[i][:, part, :],
+                    in0=units[i][:, part, :],
+                    scalar=scales[i][1][:, part : part + 1],
+                    in1=affine[:, 1, :],
+                    op0=ALU.mult,
+                    op1=ALU.add,
+                )
+                nc.sync.dma_start(out=out_rows[part][:, i, :], in_=units[i][:, part, :])
 
             sine_and_cosine(0)
             count_turns(1)
-            negate_whole(1)
+            multiply(2)
             for step in range(0, TILES + 2):
+                if 0 <= step + 1 < TILES:
+                    negate_whole(step + 1)
                 if 0 <= step < TILES:
                     open_planes(step)
-                if 0 <= step < TILES:
-                    product_of_gpsimd(step, 0, slice(0, BANKS))
+                    product_of_vector(step, 3, slice(0, BANKS))
+                    hold_gpsimd(step)
                 if 0 <= step - 2 < TILES:
                     row_moments(step - 2)
-                if 0 <= step - 2 < TILES:
-                    inverse_deviation(step - 2)
-                if 0 <= step < TILES:
-                    product_of_gpsimd(step, 1, slice(0, BANKS))
-                if 0 <= step < TILES:
-                    product_of_gpsimd(step, 2, slice(0, 1))
                 if 0 <= step - 1 < TILES:
-                    rotate(step - 1, 0)
+                    add_products(step - 1, 0, 0)
+                    add_products(step - 1, 0, 1)
                 if 0 <= step + 1 < TILES:
                     fraction(step + 1)
                 if 0 <= step < TILES:
-                    product_of_vector(step, 3, slice(0, BANKS))
-                if 0 <= step < TILES:
-                    product_of_vector(step, 2, slice(1, 2))
+                    product_of_gpsimd(step, 0, slice(0, BANKS))
+                if 0 <= step - 2 < TILES:
+                    inverse_deviation(step - 2)
+                    norm_first(step - 2, 0)
                 if 0 <= step - 1 < TILES:
-                    rotate(step - 1, 1)
-                if 0 <= step - 1 < TILES:
-                    join_totals(step - 1)
-                if 0 <= step + 1 < TILES:
-                    sine_and_cosine(step + 1)
-                if 0 <= step + 2 < TILES:
-                    multiply(step + 2)
+                    normalise(step - 1, 0, 0)
+                    normalise(step - 1, 0, 1)
+                if 0 <= step - 2 < TILES:
+                    norm_first(step - 2, 1)
                 if 0 <= step + 2 < TILES:
                     count_turns(step + 2)
-                if 0 <= step + 2 < TILES:
-                    negate_whole(step + 2)
+                if 0 <= step < TILES:
+                    product_of_gpsimd(step, 1, slice(0, BANKS))
+                    product_of_gpsimd(step, 2, slice(0, BANKS))
+                if 0 <= step - 1 < TILES:
+                    add_products(step - 1, 1, 0)
+                    add_products(step - 1, 1, 1)
                 if 0 <= step - 2 < TILES:
-                    layer_norms(step - 2)
+                    norm_second(step - 2, 0)
+                if 0 <= step - 1 < TILES:
+                    normalise(step - 1, 1, 0)
+                    normalise(step - 1, 1, 1)
+                    join_totals(step - 1)
+                if 0 <= step - 2 < TILES:
+                    norm_second(step - 2, 1)
+                if 0 <= step + 1 < TILES:
+                    sine_and_cosine(step + 1)
+                if 0 <= step + 3 < TILES:
+                    multiply(step + 3)

@@ -57,8 +57,7 @@ def tile_quantumcoherencelayer_kernel(
         tiny = whole.enter_context(tc.tile_pool(name="tiny", bufs=3))
 
         x_turned = [
-            keep.tile([P, 2, K_PASSES, P, 2], F32, name="x_turned%d" % i, align_bytes=64)
-            for i in range(TILES)
+            keep.tile([P, 2, 2 * K_PASSES, P], F32, name="x_turned%d" % i) for i in range(TILES)
         ]
         inv_n = [keep.tile([P, D], F32, name="inv_n%d" % i) for i in range(TILES)]
         x_codes = [
@@ -75,7 +74,7 @@ def tile_quantumcoherencelayer_kernel(
         psum = whole.enter_context(tc.psum_pool(name="psum", bufs=2))
         affine = psum.tile([P, 2, D], BF16, name="affine", bufs=1)
         turns = [
-            [keep.tile([P, SUBS, BANKS, P], F32, name="turns%d%d" % (turn, which)) for which in range(2)]
+            [keep.tile([P, BANKS, SUBS, P], F32, name="turns%d%d" % (turn, which)) for which in range(2)]
             for turn in range(2)
         ]
         products = {}
@@ -83,6 +82,7 @@ def tile_quantumcoherencelayer_kernel(
 
         x_tiles = {}
         words = {}
+        grouped_words = {}
         squares = {}
         part_sums = {}
         square_sums = {}
@@ -159,7 +159,7 @@ def tile_quantumcoherencelayer_kernel(
                 op0=ALU.mult,
             )
 
-            ln_rows = work1.tile([P, 2, D], BF16, name="ln_rows", bufs=1)
+            ln_rows = work1.tile([P, 2, D], BF16, name="inv_r_turned")
             nc.gpsimd.memset(ln_rows[:], 0.0)
             nc.sync.dma_start(out=ln_rows[0:1, 0, :], in_=ln_weight.rearrange("(o d) -> o d", o=1))
             nc.sync.dma_start(out=ln_rows[0:1, 1, :], in_=ln_bias.rearrange("(o d) -> o d", o=1))
@@ -188,18 +188,22 @@ def tile_quantumcoherencelayer_kernel(
                             )
                     words[i, part] = xt
 
-            def keep_words(i):
+            def group_words(i):
+                grouped = work1.tile([P, K_PASSES, P, 2], F32, name="grouped", align_bytes=64)
+                nc.scalar.copy(
+                    out=grouped[:], in_=words[i, 0][:].rearrange("p (g u) r -> p g r u", u=2)
+                )
+                grouped_words[i] = grouped
+
+            def keep_turned(i):
                 for part in range(2):
-                    nc.vector.tensor_copy(
-                        out=x_turned[i][:, part],
-                        in_=words[i, part][:].rearrange("p (g u) r -> p g r u", u=2),
-                    )
+                    nc.vector.tensor_copy(out=x_turned[i][:, part], in_=words[i, part][:])
 
             def quantise(i):
                 nc.vector.quantize_mx(
                     out=x_codes[i][:].bitcast(FP8X4),
                     scales=x_scales[i][:],
-                    in_=x_turned[i][:, 0].rearrange("p g r u -> p (g r u)").bitcast(BF16),
+                    in_=grouped_words[i][:].rearrange("p g r u -> p (g r u)").bitcast(BF16),
                 )
 
             def square(i):
@@ -324,10 +328,10 @@ def tile_quantumcoherencelayer_kernel(
                 for b in range(BANKS):
                     by_sub = products[i, b][:].rearrange("p (q t) -> p t q", t=SUBS)
                     nc.scalar.activation(
-                        out=angle[:, :, b, :], in_=by_sub, func=ACT.Copy, scale=turns_gain[:, i : i + 1]
+                        out=angle[:, b], in_=by_sub, func=ACT.Copy, scale=turns_gain[:, i : i + 1]
                     )
                     nc.scalar.activation(
-                        out=whole[:, :, b, :],
+                        out=whole[:, b],
                         in_=by_sub,
                         func=ACT.Identity,
                         scale=turns_gain[:, i : i + 1],
@@ -352,7 +356,7 @@ def tile_quantumcoherencelayer_kernel(
                         for which in range(2):
                             nc.tensor.matmul(
                                 out=frac[:, t, :],
-                                lhsT=turns[i % 2][which][:, t, b, :],
+                                lhsT=turns[i % 2][which][:, b, t, :],
                                 rhs=ident[:],
                                 is_transpose=True,
                                 start=(which == 0),
@@ -376,7 +380,8 @@ def tile_quantumcoherencelayer_kernel(
                 if 0 <= step - 2:
                     add_phases(step - 2)
                 if step < TILES:
-                    keep_words(step)
+                    group_words(step)
+                    keep_turned(step)
                 if step == GAIN_BATCH + 1:
                     coherence_gains(0)
                 if step == TILES:
@@ -404,12 +409,15 @@ def tile_quantumcoherencelayer_kernel(
             scales = {}
 
             def sine_and_cosine(i):
-                phasor = work2.tile([P, 2, SUBS, BANKS, P], F32, name="phasor")
+                phasor = work2.tile([P, 2, D], F32, name="phasor")
                 for b in range(BANKS):
-                    nc.scalar.activation(out=phasor[:, 0, :, b, :], in_=fractions[i, b][:], func=ACT.Abs)
-                    nc.scalar.activation(
-                        out=phasor[:, 1, :, b, :], in_=fractions[i, b][:], func=ACT.Sin, scale=2.0 * math.pi
-                    )
+                    ordered = fractions[i, b][:].rearrange("p (u h) r -> p u r h", h=2)
+                    absolute, sine = [
+                        phasor[:, which, HALF * b : HALF * (b + 1)].rearrange("p (u r h) -> p u r h", u=2, h=2)
+                        for which in range(2)
+                    ]
+                    nc.scalar.activation(out=absolute, in_=ordered, func=ACT.Abs)
+                    nc.scalar.activation(out=sine, in_=ordered, func=ACT.Sin, scale=2.0 * math.pi)
                 nc.scalar.activation(
                     out=phasor[:, 0],
                     in_=phasor[:, 0],
@@ -419,39 +427,34 @@ def tile_quantumcoherencelayer_kernel(
                 )
                 phasors[i] = phasor
 
-            def turned_part(i, part):
-                return (
-                    x_turned[i][:, part]
-                    .rearrange("p g r u -> p (g r u)")
-                    .bitcast(BF16)
-                    .rearrange("p (g r t) -> p t g r", g=K_PASSES, t=SUBS)
-                )
-
             def open_planes(i):
                 for which in (3, 0, 1, 2):
-                    planes[i, which] = work2.tile([P, SUBS, BANKS, P], F32, name="plane", bufs=PLANES)
+                    planes[i, which] = work2.tile([P, D], F32, name="plane", bufs=PLANES)
                 rotated[i] = ((planes[i, 0], planes[i, 3]), (planes[i, 1], planes[i, 2]))
+
+            def turned_part(i, which):
+                return x_turned[i][:, which // 2].rearrange("p w r -> p (w r)").bitcast(BF16)
 
             def product_of_gpsimd(i, which, banks):
                 nc.gpsimd.tensor_tensor(
-                    out=planes[i, which][:, :, banks, :],
-                    in0=turned_part(i, which // 2)[:, :, banks, :],
-                    in1=phasors[i][:, which % 2, :, banks, :],
+                    out=planes[i, which][:, banks],
+                    in0=turned_part(i, which)[:, banks],
+                    in1=phasors[i][:, which % 2, banks],
                     op=ALU.mult,
                 )
 
             def product_of_vector(i, which, banks):
                 nc.vector.scalar_tensor_tensor(
-                    out=planes[i, which][:, :, banks, :],
-                    in0=turned_part(i, which // 2)[:, :, banks, :],
+                    out=planes[i, which][:, banks],
+                    in0=turned_part(i, which)[:, banks],
                     scalar=-1.0 if which == 3 else 1.0,
-                    in1=phasors[i][:, which % 2, :, banks, :],
+                    in1=phasors[i][:, which % 2, banks],
                     op0=ALU.mult,
                     op1=ALU.mult,
                 )
 
             def hold_gpsimd(i):
-                nc.vector.memset(planes[i, 0][:, 0, 0, 0:1], 0.0)
+                nc.vector.memset(planes[i, 0][:, 0:1], 0.0)
 
             def add_products(i, part, b):
                 rows = psum.tile([P, SUBS, P], F32, name="ring_c")
@@ -459,7 +462,7 @@ def tile_quantumcoherencelayer_kernel(
                     for which in range(2):
                         nc.tensor.matmul(
                             out=rows[:, t, :],
-                            lhsT=rotated[i][part][which][:, t, b, :],
+                            lhsT=rotated[i][part][which][:, HALF * b + 2 * P * (t // 2) + t % 2 : HALF * b + 2 * P * (t // 2 + 1) : 2],
                             rhs=ident[:],
                             is_transpose=True,
                             start=(which == 0),
@@ -557,7 +560,7 @@ def tile_quantumcoherencelayer_kernel(
                     negate_whole(step + 1)
                 if 0 <= step < TILES:
                     open_planes(step)
-                    product_of_vector(step, 3, slice(0, BANKS))
+                    product_of_vector(step, 3, slice(0, D))
                     hold_gpsimd(step)
                 if 0 <= step - 2 < TILES:
                     row_moments(step - 2)
@@ -567,7 +570,7 @@ def tile_quantumcoherencelayer_kernel(
                 if 0 <= step + 1 < TILES:
                     fraction(step + 1)
                 if 0 <= step < TILES:
-                    product_of_gpsimd(step, 0, slice(0, BANKS))
+                    product_of_gpsimd(step, 0, slice(0, D))
                 if 0 <= step - 2 < TILES:
                     inverse_deviation(step - 2)
                     norm_first(step - 2, 0)
@@ -579,8 +582,8 @@ def tile_quantumcoherencelayer_kernel(
                 if 0 <= step + 2 < TILES:
                     count_turns(step + 2)
                 if 0 <= step < TILES:
-                    product_of_gpsimd(step, 1, slice(0, BANKS))
-                    product_of_gpsimd(step, 2, slice(0, BANKS))
+                    product_of_gpsimd(step, 1, slice(0, D))
+                    product_of_gpsimd(step, 2, slice(0, D))
                 if 0 <= step - 1 < TILES:
                     add_products(step - 1, 1, 0)
                     add_products(step - 1, 1, 1)

@@ -326,12 +326,12 @@ def tile_quantumcoherencelayer_kernel(
             def count_turns(i):
                 angle, whole = turns[i % 2]
                 for b in range(BANKS):
-                    by_sub = products[i, b][:].rearrange("p (q t) -> p t q", t=SUBS)
+                    by_sub = products[i, b][:].rearrange("p (q t) -> p q t", t=SUBS)
                     nc.scalar.activation(
-                        out=angle[:, b], in_=by_sub, func=ACT.Copy, scale=turns_gain[:, i : i + 1]
+                        out=angle[:, b].rearrange("p t q -> p q t"), in_=by_sub, func=ACT.Copy, scale=turns_gain[:, i : i + 1]
                     )
                     nc.scalar.activation(
-                        out=whole[:, b],
+                        out=whole[:, b].rearrange("p t q -> p q t"),
                         in_=by_sub,
                         func=ACT.Identity,
                         scale=turns_gain[:, i : i + 1],
@@ -369,14 +369,21 @@ def tile_quantumcoherencelayer_kernel(
                     add_shift(step - 1)
                 if 0 <= step - 2:
                     turn_back(step - 2)
+                if step == TILES - 1:
+                    multiply(0)
                 if step < TILES:
-                    turn_words(step)
                     square(step)
                     add_parts(step)
+                if step == TILES - 1:
+                    count_turns(0)
+                if step < TILES:
+                    turn_words(step)
                 if 0 <= step - 1 < TILES:
                     root_n(step - 1)
                     root_r(step - 1)
                     quantise(step - 1)
+                if step == TILES:
+                    negate_whole(0)
                 if 0 <= step - 2:
                     add_phases(step - 2)
                 if step < TILES:
@@ -385,12 +392,9 @@ def tile_quantumcoherencelayer_kernel(
                 if step == GAIN_BATCH + 1:
                     coherence_gains(0)
                 if step == TILES:
-                    multiply(0)
-                    count_turns(0)
-                    negate_whole(0)
                     nc.scalar.activation(out=warm_up[:], in_=ones[:], func=ACT.Sin)
-                if step == TILES + 1:
                     fraction(0)
+                if step == TILES + 1:
                     coherence_gains(GAIN_BATCH)
                     multiply(1)
                 if step + 2 < TILES:
@@ -457,11 +461,11 @@ def tile_quantumcoherencelayer_kernel(
                 nc.vector.memset(planes[i, 0][:, 0:1], 0.0)
 
             def add_products(i, part, b):
-                rows = psum.tile([P, SUBS, P], F32, name="ring_c")
+                rows = psum.tile([P, HALF], F32, name="ring_c")
                 for t in range(SUBS):
                     for which in range(2):
                         nc.tensor.matmul(
-                            out=rows[:, t, :],
+                            out=rows[:, t::SUBS],
                             lhsT=rotated[i][part][which][:, HALF * b + 2 * P * (t // 2) + t % 2 : HALF * b + 2 * P * (t // 2 + 1) : 2],
                             rhs=ident[:],
                             is_transpose=True,
@@ -475,12 +479,10 @@ def tile_quantumcoherencelayer_kernel(
                     units[i] = work2.tile([P, 2, D], F32, name="unit", bufs=3)
                     totals[i] = tiny.tile([P, 2, BANKS], F32, name="total")
                 nc.vector.scalar_tensor_tensor(
-                    out=units[i][:, part, HALF * b : HALF * (b + 1)].rearrange(
-                        "p (q t) -> p q t", t=SUBS
-                    ),
-                    in0=rotated_rows[i, part, b][:].rearrange("p t q -> p q t"),
+                    out=units[i][:, part, HALF * b : HALF * (b + 1)],
+                    in0=rotated_rows[i, part, b][:],
                     scalar=1.0,
-                    in1=inv_n[i][:, HALF * b : HALF * (b + 1)].rearrange("p (q t) -> p q t", t=SUBS),
+                    in1=inv_n[i][:, HALF * b : HALF * (b + 1)],
                     op0=ALU.mult,
                     op1=ALU.mult,
                     accum_out=totals[i][:, part, b : b + 1],
@@ -556,11 +558,12 @@ def tile_quantumcoherencelayer_kernel(
             count_turns(1)
             multiply(2)
             for step in range(0, TILES + 2):
-                if 0 <= step + 1 < TILES:
-                    negate_whole(step + 1)
                 if 0 <= step < TILES:
                     open_planes(step)
                     product_of_vector(step, 3, slice(0, D))
+                if 0 <= step + 1 < TILES:
+                    negate_whole(step + 1)
+                if 0 <= step < TILES:
                     hold_gpsimd(step)
                 if 0 <= step - 2 < TILES:
                     row_moments(step - 2)

@@ -561,6 +561,7 @@ def tile_quantumcoherencelayer_kernel(
                 if 0 <= step < TILES:
                     open_planes(step)
                     product_of_vector(step, 3, slice(0, D))
+                    product_of_vector(step, 2, slice(0, D))
                 if 0 <= step + 1 < TILES:
                     negate_whole(step + 1)
                 if 0 <= step < TILES:
@@ -586,7 +587,6 @@ def tile_quantumcoherencelayer_kernel(
                     count_turns(step + 2)
                 if 0 <= step < TILES:
                     product_of_gpsimd(step, 1, slice(0, D))
-                    product_of_gpsimd(step, 2, slice(0, D))
                 if 0 <= step - 1 < TILES:
                     add_products(step - 1, 1, 0)
                     add_products(step - 1, 1, 1)

@@ -27,7 +27,7 @@ EPS = 1e-8
 ROUND_MAGIC = 12582912.0
 SUBS = 4
 GAIN_BATCH = 8
-PLANES = 6
+PLANES = 8
 SQUARE_SCALE = math.sqrt(1.0 / (2.0 * EPS))
 
 FLOPS = 2 * ROWS * D * D
@@ -56,8 +56,8 @@ def tile_quantumcoherencelayer_kernel(
         keep = whole.enter_context(tc.tile_pool(name="keep", bufs=1))
         tiny = whole.enter_context(tc.tile_pool(name="tiny", bufs=3))
 
-        x_turned = [
-            keep.tile([P, 2, 2 * K_PASSES, P], F32, name="x_turned%d" % i) for i in range(TILES)
+        imag_words = [
+            keep.tile([P, 2 * K_PASSES, P], F32, name="imag_words%d" % i) for i in range(TILES)
         ]
         inv_n = [keep.tile([P, D], F32, name="inv_n%d" % i) for i in range(TILES)]
         x_codes = [
@@ -90,7 +90,7 @@ def tile_quantumcoherencelayer_kernel(
         inv_r_turned = {}
         inv_r = {}
 
-        with tc.tile_pool(name="x_in", bufs=4) as x_in, tc.tile_pool(
+        with tc.tile_pool(name="x_in", bufs=5) as x_in, tc.tile_pool(
             name="work1", bufs=2
         ) as work1:
 
@@ -159,7 +159,7 @@ def tile_quantumcoherencelayer_kernel(
                 op0=ALU.mult,
             )
 
-            ln_rows = work1.tile([P, 2, D], BF16, name="inv_r_turned")
+            ln_rows = work1.tile([P, 2, D], BF16, name="ln_rows", bufs=1)
             nc.gpsimd.memset(ln_rows[:], 0.0)
             nc.sync.dma_start(out=ln_rows[0:1, 0, :], in_=ln_weight.rearrange("(o d) -> o d", o=1))
             nc.sync.dma_start(out=ln_rows[0:1, 1, :], in_=ln_bias.rearrange("(o d) -> o d", o=1))
@@ -196,8 +196,13 @@ def tile_quantumcoherencelayer_kernel(
                 grouped_words[i] = grouped
 
             def keep_turned(i):
-                for part in range(2):
-                    nc.vector.tensor_copy(out=x_turned[i][:, part], in_=words[i, part][:])
+                turned = work1.tile([P, D], F32, name="turned")
+                nc.vector.tensor_copy(
+                    out=turned[:],
+                    in_=words[i, 0][:].rearrange("p w r -> p (w r)").bitcast(BF16),
+                )
+                nc.sync.dma_start(out=out_rows[0][:, i, :], in_=turned[:])
+                nc.vector.tensor_copy(out=imag_words[i][:], in_=words[i, 1][:])
 
             def quantise(i):
                 nc.vector.quantize_mx(
@@ -338,9 +343,15 @@ def tile_quantumcoherencelayer_kernel(
                         bias=magic[:],
                     )
 
+            def negate_first(i):
+                whole = turns[i % 2][1]
+                nc.scalar.activation(
+                    out=whole[:], in_=whole[:], func=ACT.Identity, scale=-1.0, bias=magic[:]
+                )
+
             def negate_whole(i):
                 whole = turns[i % 2][1]
-                nc.vector.tensor_scalar(
+                nc.gpsimd.tensor_scalar(
                     out=whole[:],
                     in0=whole[:],
                     scalar1=-1.0,
@@ -365,6 +376,8 @@ def tile_quantumcoherencelayer_kernel(
                     fractions[i, b] = frac
 
             for step in range(TILES + 2):
+                if step + 2 < TILES:
+                    load(step + 2)
                 if 0 <= step - 1 < TILES:
                     add_shift(step - 1)
                 if 0 <= step - 2:
@@ -374,13 +387,14 @@ def tile_quantumcoherencelayer_kernel(
                 if step < TILES:
                     square(step)
                     add_parts(step)
-                if step == TILES - 1:
-                    count_turns(0)
                 if step < TILES:
                     turn_words(step)
                 if 0 <= step - 1 < TILES:
                     root_n(step - 1)
                     root_r(step - 1)
+                if step == TILES - 1:
+                    count_turns(0)
+                if 0 <= step - 1 < TILES:
                     quantise(step - 1)
                 if step == TILES:
                     negate_whole(0)
@@ -395,14 +409,12 @@ def tile_quantumcoherencelayer_kernel(
                     nc.scalar.activation(out=warm_up[:], in_=ones[:], func=ACT.Sin)
                     fraction(0)
                 if step == TILES + 1:
-                    coherence_gains(GAIN_BATCH)
                     multiply(1)
-                if step + 2 < TILES:
-                    load(step + 2)
-                if step == 1:
+                if step == GAIN_BATCH:
                     spread_affine()
 
         with tc.tile_pool(name="work2", bufs=2, reuse_waits="tile") as work2:
+            real_turned = {}
             phasors = {}
             planes = {}
             rotated = {}
@@ -436,8 +448,14 @@ def tile_quantumcoherencelayer_kernel(
                     planes[i, which] = work2.tile([P, D], F32, name="plane", bufs=PLANES)
                 rotated[i] = ((planes[i, 0], planes[i, 3]), (planes[i, 1], planes[i, 2]))
 
+            def fetch_turned(i):
+                real_turned[i] = work2.tile([P, D], F32, name="real_turned", bufs=3)
+                nc.sync.dma_start(out=real_turned[i][:], in_=out_rows[0][:, i, :])
+
             def turned_part(i, which):
-                return x_turned[i][:, which // 2].rearrange("p w r -> p (w r)").bitcast(BF16)
+                if which < 2:
+                    return real_turned[i][:]
+                return imag_words[i][:].rearrange("p w r -> p (w r)").bitcast(BF16)
 
             def product_of_gpsimd(i, which, banks):
                 nc.gpsimd.tensor_tensor(
@@ -476,7 +494,7 @@ def tile_quantumcoherencelayer_kernel(
 
             def normalise(i, part, b):
                 if (part, b) == (0, 0):
-                    units[i] = work2.tile([P, 2, D], F32, name="unit", bufs=3)
+                    units[i] = work2.tile([P, 2, D], F32, name="unit", bufs=4)
                     totals[i] = tiny.tile([P, 2, BANKS], F32, name="total")
                 nc.vector.scalar_tensor_tensor(
                     out=units[i][:, part, HALF * b : HALF * (b + 1)],
@@ -488,19 +506,17 @@ def tile_quantumcoherencelayer_kernel(
                     accum_out=totals[i][:, part, b : b + 1],
                 )
 
-            row_totals = {}
-
-            def join_totals(i):
-                row_total = tiny.tile([P, 2], F32, name="row_total")
-                nc.vector.tensor_tensor(
-                    out=row_total[:], in0=totals[i][:, :, 0], in1=totals[i][:, :, 1], op=ALU.add
-                )
-                row_totals[i] = row_total
-
             def row_moments(i):
-                total = row_totals[i]
+                shares = tiny.tile([P, 2, BANKS], F32, name="shares")
+                nc.scalar.activation(out=shares[:], in_=totals[i][:], func=ACT.Copy, scale=1.0 / D)
                 mean = tiny.tile([P, 2], F32, name="mean")
-                nc.scalar.activation(out=mean[:], in_=total[:], func=ACT.Copy, scale=1.0 / D)
+                for part in range(2):
+                    nc.scalar.activation(
+                        out=mean[:, part : part + 1],
+                        in_=shares[:, part, 0:1],
+                        func=ACT.Identity,
+                        bias=shares[:, part, 1:2],
+                    )
                 total_sq = tiny.tile([P, 2], F32, name="total_sq")
                 for part in range(2):
                     unread = work2.tile([P, D], BF16, name="unread_sq", bufs=1)
@@ -511,7 +527,7 @@ def tile_quantumcoherencelayer_kernel(
                         accum_out=total_sq[:, part : part + 1],
                     )
                 mean_sq = tiny.tile([P, 2], F32, name="mean_sq")
-                nc.scalar.activation(out=mean_sq[:], in_=total[:], func=ACT.Square, scale=1.0 / D)
+                nc.scalar.activation(out=mean_sq[:], in_=mean[:], func=ACT.Square)
                 shift = tiny.tile([P, 2], F32, name="shift")
                 nc.scalar.activation(
                     out=shift[:], in_=mean_sq[:], func=ACT.Identity, scale=-1.0, bias=eps[:]
@@ -554,18 +570,19 @@ def tile_quantumcoherencelayer_kernel(
                 )
                 nc.sync.dma_start(out=out_rows[part][:, i, :], in_=units[i][:, part, :])
 
+            fetch_turned(0)
+            fetch_turned(1)
             sine_and_cosine(0)
             count_turns(1)
+            negate_first(1)
             multiply(2)
             for step in range(0, TILES + 2):
+                if 0 <= step + 2 < TILES:
+                    fetch_turned(step + 2)
                 if 0 <= step < TILES:
                     open_planes(step)
                     product_of_vector(step, 3, slice(0, D))
-                    product_of_vector(step, 2, slice(0, D))
-                if 0 <= step + 1 < TILES:
-                    negate_whole(step + 1)
-                if 0 <= step < TILES:
-                    hold_gpsimd(step)
+                    product_of_vector(step, 2, slice(HALF, D))
                 if 0 <= step - 2 < TILES:
                     row_moments(step - 2)
                 if 0 <= step - 1 < TILES:
@@ -577,25 +594,31 @@ def tile_quantumcoherencelayer_kernel(
                     product_of_gpsimd(step, 0, slice(0, D))
                 if 0 <= step - 2 < TILES:
                     inverse_deviation(step - 2)
-                    norm_first(step - 2, 0)
                 if 0 <= step - 1 < TILES:
                     normalise(step - 1, 0, 0)
+                if 0 <= step - 2 < TILES:
+                    norm_first(step - 2, 0)
+                if 0 <= step - 1 < TILES:
                     normalise(step - 1, 0, 1)
                 if 0 <= step - 2 < TILES:
                     norm_first(step - 2, 1)
+                if step == 1:
+                    coherence_gains(GAIN_BATCH)
                 if 0 <= step + 2 < TILES:
                     count_turns(step + 2)
                 if 0 <= step < TILES:
                     product_of_gpsimd(step, 1, slice(0, D))
+                    product_of_gpsimd(step, 2, slice(0, HALF))
+                if 0 <= step + 2 < TILES:
+                    negate_whole(step + 2)
                 if 0 <= step - 1 < TILES:
                     add_products(step - 1, 1, 0)
                     add_products(step - 1, 1, 1)
+                    normalise(step - 1, 1, 0)
                 if 0 <= step - 2 < TILES:
                     norm_second(step - 2, 0)
                 if 0 <= step - 1 < TILES:
-                    normalise(step - 1, 1, 0)
                     normalise(step - 1, 1, 1)
-                    join_totals(step - 1)
                 if 0 <= step - 2 < TILES:
                     norm_second(step - 2, 1)
                 if 0 <= step + 1 < TILES:

@@ -27,6 +27,7 @@ EPS = 1e-8
 ROUND_MAGIC = 12582912.0
 SUBS = 4
 GAIN_BATCH = 8
+RESIDENT = 3
 PLANES = 8
 SQUARE_SCALE = math.sqrt(1.0 / (2.0 * EPS))
 
@@ -79,6 +80,9 @@ def tile_quantumcoherencelayer_kernel(
         ]
         products = {}
         fractions = {}
+
+        keep_ring = whole.enter_context(tc.tile_pool(name="keep_ring", bufs=RESIDENT))
+        real_turned = {}
 
         x_tiles = {}
         words = {}
@@ -196,12 +200,16 @@ def tile_quantumcoherencelayer_kernel(
                 grouped_words[i] = grouped
 
             def keep_turned(i):
-                turned = work1.tile([P, D], F32, name="turned")
+                resident = i < RESIDENT
+                turned = (keep_ring if resident else work1).tile([P, D], F32, name="real_turned")
                 nc.vector.tensor_copy(
                     out=turned[:],
                     in_=words[i, 0][:].rearrange("p w r -> p (w r)").bitcast(BF16),
                 )
-                nc.sync.dma_start(out=out_rows[0][:, i, :], in_=turned[:])
+                if resident:
+                    real_turned[i] = turned
+                else:
+                    nc.sync.dma_start(out=out_rows[0][:, i, :], in_=turned[:])
                 nc.vector.tensor_copy(out=imag_words[i][:], in_=words[i, 1][:])
 
             def quantise(i):
@@ -413,8 +421,9 @@ def tile_quantumcoherencelayer_kernel(
                 if step == GAIN_BATCH:
                     spread_affine()
 
-        with tc.tile_pool(name="work2", bufs=2, reuse_waits="tile") as work2:
-            real_turned = {}
+        with tc.tile_pool(name="late", bufs=4, reuse_waits="tile") as late, tc.tile_pool(
+            name="work2", bufs=2, reuse_waits="tile"
+        ) as work2:
             phasors = {}
             planes = {}
             rotated = {}
@@ -422,7 +431,6 @@ def tile_quantumcoherencelayer_kernel(
             units = {}
             totals = {}
             moments = {}
-            scales = {}
 
             def sine_and_cosine(i):
                 phasor = work2.tile([P, 2, D], F32, name="phasor")
@@ -449,8 +457,9 @@ def tile_quantumcoherencelayer_kernel(
                 rotated[i] = ((planes[i, 0], planes[i, 3]), (planes[i, 1], planes[i, 2]))
 
             def fetch_turned(i):
-                real_turned[i] = work2.tile([P, D], F32, name="real_turned", bufs=3)
-                nc.sync.dma_start(out=real_turned[i][:], in_=out_rows[0][:, i, :])
+                if i >= RESIDENT:
+                    real_turned[i] = keep_ring.tile([P, D], F32, name="real_turned")
+                    nc.sync.dma_start(out=real_turned[i][:], in_=out_rows[0][:, i, :])
 
             def turned_part(i, which):
                 if which < 2:
@@ -494,7 +503,7 @@ def tile_quantumcoherencelayer_kernel(
 
             def normalise(i, part, b):
                 if (part, b) == (0, 0):
-                    units[i] = work2.tile([P, 2, D], F32, name="unit", bufs=4)
+                    units[i] = late.tile([P, 2, D], F32, name="unit")
                     totals[i] = tiny.tile([P, 2, BANKS], F32, name="total")
                 nc.vector.scalar_tensor_tensor(
                     out=units[i][:, part, HALF * b : HALF * (b + 1)],
@@ -506,11 +515,17 @@ def tile_quantumcoherencelayer_kernel(
                     accum_out=totals[i][:, part, b : b + 1],
                 )
 
-            def row_moments(i):
+            def open_moments(i):
+                moments[i] = [tiny.tile([P, 2], F32, name=name) for name in ("mean", "spread", "rstd")]
+
+            def row_moments(i, parts):
+                mean, spread = moments[i][0:2]
                 shares = tiny.tile([P, 2, BANKS], F32, name="shares")
-                nc.scalar.activation(out=shares[:], in_=totals[i][:], func=ACT.Copy, scale=1.0 / D)
-                mean = tiny.tile([P, 2], F32, name="mean")
-                for part in range(2):
+                nc.scalar.activation(
+                    out=shares[:, parts, :], in_=totals[i][:, parts, :], func=ACT.Copy, scale=1.0 / D
+                )
+                each = range(parts.start, parts.stop)
+                for part in each:
                     nc.scalar.activation(
                         out=mean[:, part : part + 1],
                         in_=shares[:, part, 0:1],
@@ -518,7 +533,7 @@ def tile_quantumcoherencelayer_kernel(
                         bias=shares[:, part, 1:2],
                     )
                 total_sq = tiny.tile([P, 2], F32, name="total_sq")
-                for part in range(2):
+                for part in each:
                     unread = work2.tile([P, D], BF16, name="unread_sq", bufs=1)
                     nc.scalar.activation(
                         out=unread[:],
@@ -527,13 +542,12 @@ def tile_quantumcoherencelayer_kernel(
                         accum_out=total_sq[:, part : part + 1],
                     )
                 mean_sq = tiny.tile([P, 2], F32, name="mean_sq")
-                nc.scalar.activation(out=mean_sq[:], in_=mean[:], func=ACT.Square)
+                nc.scalar.activation(out=mean_sq[:, parts], in_=mean[:, parts], func=ACT.Square)
                 shift = tiny.tile([P, 2], F32, name="shift")
                 nc.scalar.activation(
-                    out=shift[:], in_=mean_sq[:], func=ACT.Identity, scale=-1.0, bias=eps[:]
+                    out=shift[:, parts], in_=mean_sq[:, parts], func=ACT.Identity, scale=-1.0, bias=eps[:]
                 )
-                spread = tiny.tile([P, 2], F32, name="spread")
-                for part in range(2):
+                for part in each:
                     nc.scalar.activation(
                         out=spread[:, part : part + 1],
                         in_=total_sq[:, part : part + 1],
@@ -541,13 +555,12 @@ def tile_quantumcoherencelayer_kernel(
                         scale=1.0 / D,
                         bias=shift[:, part : part + 1],
                     )
-                moments[i] = (mean, spread)
 
-            def inverse_deviation(i):
-                mean, spread = moments[i]
-                rstd = tiny.tile([P, 2], F32, name="rstd")
-                nc.gpsimd.tensor_tensor(out=rstd[:], in0=spread[:], in1=minus_half[:], op=ALU.pow)
-                scales[i] = (mean, rstd)
+            def inverse_deviation(i, parts):
+                mean, spread, rstd = moments[i]
+                nc.gpsimd.tensor_tensor(
+                    out=rstd[:, parts], in0=spread[:, parts], in1=minus_half[:, parts], op=ALU.pow
+                )
 
             def norm_first(i, part):
                 nc.vector.scalar_tensor_tensor(
@@ -563,15 +576,16 @@ def tile_quantumcoherencelayer_kernel(
                 nc.vector.scalar_tensor_tensor(
                     out=units[i][:, part, :],
                     in0=units[i][:, part, :],
-                    scalar=scales[i][1][:, part : part + 1],
+                    scalar=moments[i][2][:, part : part + 1],
                     in1=affine[:, 1, :],
                     op0=ALU.mult,
                     op1=ALU.add,
                 )
                 nc.sync.dma_start(out=out_rows[part][:, i, :], in_=units[i][:, part, :])
 
-            fetch_turned(0)
-            fetch_turned(1)
+            def gpsimd_share(i):
+                return HALF if i < TILES - 1 else 0
+
             sine_and_cosine(0)
             count_turns(1)
             negate_first(1)
@@ -582,46 +596,47 @@ def tile_quantumcoherencelayer_kernel(
                 if 0 <= step < TILES:
                     open_planes(step)
                     product_of_vector(step, 3, slice(0, D))
-                    product_of_vector(step, 2, slice(HALF, D))
-                if 0 <= step - 2 < TILES:
-                    row_moments(step - 2)
+                    product_of_vector(step, 2, slice(gpsimd_share(step), D))
+                    hold_gpsimd(step)
+                    product_of_gpsimd(step, 0, slice(0, D))
                 if 0 <= step - 1 < TILES:
-                    add_products(step - 1, 0, 0)
-                    add_products(step - 1, 0, 1)
+                    add_products(step - 1, 1, 0)
+                    add_products(step - 1, 1, 1)
                 if 0 <= step + 1 < TILES:
                     fraction(step + 1)
-                if 0 <= step < TILES:
-                    product_of_gpsimd(step, 0, slice(0, D))
-                if 0 <= step - 2 < TILES:
-                    inverse_deviation(step - 2)
-                if 0 <= step - 1 < TILES:
-                    normalise(step - 1, 0, 0)
-                if 0 <= step - 2 < TILES:
-                    norm_first(step - 2, 0)
-                if 0 <= step - 1 < TILES:
-                    normalise(step - 1, 0, 1)
-                if 0 <= step - 2 < TILES:
-                    norm_first(step - 2, 1)
                 if step == 1:
                     coherence_gains(GAIN_BATCH)
                 if 0 <= step + 2 < TILES:
                     count_turns(step + 2)
-                if 0 <= step < TILES:
-                    product_of_gpsimd(step, 1, slice(0, D))
-                    product_of_gpsimd(step, 2, slice(0, HALF))
-                if 0 <= step + 2 < TILES:
-                    negate_whole(step + 2)
                 if 0 <= step - 1 < TILES:
-                    add_products(step - 1, 1, 0)
-                    add_products(step - 1, 1, 1)
                     normalise(step - 1, 1, 0)
                 if 0 <= step - 2 < TILES:
-                    norm_second(step - 2, 0)
+                    inverse_deviation(step - 2, slice(0, 2))
+                    norm_first(step - 2, 0)
                 if 0 <= step - 1 < TILES:
                     normalise(step - 1, 1, 1)
                 if 0 <= step - 2 < TILES:
-                    norm_second(step - 2, 1)
+                    norm_first(step - 2, 1)
                 if 0 <= step + 1 < TILES:
                     sine_and_cosine(step + 1)
+                if 0 <= step - 1 < TILES:
+                    open_moments(step - 1)
+                    row_moments(step - 1, slice(0, 2))
+                if 0 <= step < TILES:
+                    product_of_gpsimd(step, 1, slice(0, D))
+                    if gpsimd_share(step) > 0:
+                        product_of_gpsimd(step, 2, slice(0, gpsimd_share(step)))
+                if 0 <= step + 2 < TILES:
+                    negate_whole(step + 2)
+                if 0 <= step < TILES:
+                    add_products(step, 0, 0)
+                    add_products(step, 0, 1)
                 if 0 <= step + 3 < TILES:
                     multiply(step + 3)
+                if 0 <= step - 2 < TILES:
+                    norm_second(step - 2, 0)
+                if 0 <= step < TILES:
+                    normalise(step, 0, 0)
+                    normalise(step, 0, 1)
+                if 0 <= step - 2 < TILES:
+                    norm_second(step - 2, 1)

@@ -199,12 +199,18 @@ def tile_quantumcoherencelayer_kernel(
                 )
                 grouped_words[i] = grouped
 
+            def halves(tile):
+                return tile[:].bitcast(BF16).rearrange("p w (r h) -> p w h r", h=2)
+
+            def by_half(plane):
+                return plane.rearrange("p (w h r) -> p w h r", h=2, r=P)
+
             def keep_turned(i):
                 resident = i < RESIDENT
                 turned = (keep_ring if resident else work1).tile([P, D], F32, name="real_turned")
                 nc.vector.tensor_copy(
-                    out=turned[:],
-                    in_=words[i, 0][:].rearrange("p w r -> p (w r)").bitcast(BF16),
+                    out=by_half(turned[:]),
+                    in_=halves(words[i, 0]),
                 )
                 if resident:
                     real_turned[i] = turned
@@ -435,13 +441,12 @@ def tile_quantumcoherencelayer_kernel(
             def sine_and_cosine(i):
                 phasor = work2.tile([P, 2, D], F32, name="phasor")
                 for b in range(BANKS):
-                    ordered = fractions[i, b][:].rearrange("p (u h) r -> p u r h", h=2)
-                    absolute, sine = [
-                        phasor[:, which, HALF * b : HALF * (b + 1)].rearrange("p (u r h) -> p u r h", u=2, h=2)
-                        for which in range(2)
-                    ]
-                    nc.scalar.activation(out=absolute, in_=ordered, func=ACT.Abs)
-                    nc.scalar.activation(out=sine, in_=ordered, func=ACT.Sin, scale=2.0 * math.pi)
+                    turn = fractions[i, b][:].rearrange("p t r -> p (t r)")
+                    cols = slice(HALF * b, HALF * (b + 1))
+                    nc.scalar.activation(out=phasor[:, 0, cols], in_=turn, func=ACT.Abs)
+                    nc.scalar.activation(
+                        out=phasor[:, 1, cols], in_=turn, func=ACT.Sin, scale=2.0 * math.pi
+                    )
                 nc.scalar.activation(
                     out=phasor[:, 0],
                     in_=phasor[:, 0],
@@ -461,39 +466,53 @@ def tile_quantumcoherencelayer_kernel(
                     real_turned[i] = keep_ring.tile([P, D], F32, name="real_turned")
                     nc.sync.dma_start(out=real_turned[i][:], in_=out_rows[0][:, i, :])
 
-            def turned_part(i, which):
-                if which < 2:
-                    return real_turned[i][:]
-                return imag_words[i][:].rearrange("p w r -> p (w r)").bitcast(BF16)
-
-            def product_of_gpsimd(i, which, banks):
+            def real_product(i, which):
                 nc.gpsimd.tensor_tensor(
-                    out=planes[i, which][:, banks],
-                    in0=turned_part(i, which)[:, banks],
-                    in1=phasors[i][:, which % 2, banks],
+                    out=planes[i, which][:],
+                    in0=real_turned[i][:],
+                    in1=phasors[i][:, which, :],
                     op=ALU.mult,
                 )
 
-            def product_of_vector(i, which, banks):
-                nc.vector.scalar_tensor_tensor(
-                    out=planes[i, which][:, banks],
-                    in0=turned_part(i, which)[:, banks],
-                    scalar=-1.0 if which == 3 else 1.0,
-                    in1=phasors[i][:, which % 2, banks],
-                    op0=ALU.mult,
-                    op1=ALU.mult,
+            def imag_cosine_of_gpsimd(i):
+                mine = slice(0, gpsimd_share(i))
+                nc.gpsimd.tensor_tensor(
+                    out=by_half(planes[i, 2][:])[:, mine],
+                    in0=halves(imag_words[i])[:, mine],
+                    in1=by_half(phasors[i][:, 0, :])[:, mine],
+                    op=ALU.mult,
                 )
+
+            def imag_cosine(i):
+                mine = slice(gpsimd_share(i), 2 * K_PASSES)
+                nc.vector.tensor_tensor(
+                    out=by_half(planes[i, 2][:])[:, mine],
+                    in0=halves(imag_words[i])[:, mine],
+                    in1=by_half(phasors[i][:, 0, :])[:, mine],
+                    op=ALU.mult,
+                )
+
+            def imag_sine(i):
+                for h in range(2):
+                    nc.vector.scalar_tensor_tensor(
+                        out=by_half(planes[i, 3][:])[:, :, h, :],
+                        in0=halves(imag_words[i])[:, :, h, :],
+                        scalar=-1.0,
+                        in1=by_half(phasors[i][:, 1, :])[:, :, h, :],
+                        op0=ALU.mult,
+                        op1=ALU.mult,
+                    )
 
             def hold_gpsimd(i):
                 nc.vector.memset(planes[i, 0][:, 0:1], 0.0)
 
             def add_products(i, part, b):
-                rows = psum.tile([P, HALF], F32, name="ring_c")
+                rows = psum.tile([P, SUBS, P], F32, name="ring_c")
                 for t in range(SUBS):
                     for which in range(2):
                         nc.tensor.matmul(
-                            out=rows[:, t::SUBS],
-                            lhsT=rotated[i][part][which][:, HALF * b + 2 * P * (t // 2) + t % 2 : HALF * b + 2 * P * (t // 2 + 1) : 2],
+                            out=rows[:, t, :],
+                            lhsT=rotated[i][part][which][:, HALF * b + P * t : HALF * b + P * (t + 1)],
                             rhs=ident[:],
                             is_transpose=True,
                             start=(which == 0),
@@ -505,11 +524,12 @@ def tile_quantumcoherencelayer_kernel(
                 if (part, b) == (0, 0):
                     units[i] = late.tile([P, 2, D], F32, name="unit")
                     totals[i] = tiny.tile([P, 2, BANKS], F32, name="total")
+                cols = slice(HALF * b, HALF * (b + 1))
                 nc.vector.scalar_tensor_tensor(
-                    out=units[i][:, part, HALF * b : HALF * (b + 1)],
-                    in0=rotated_rows[i, part, b][:],
+                    out=units[i][:, part, cols].rearrange("p (q t) -> p q t", t=SUBS),
+                    in0=rotated_rows[i, part, b][:].rearrange("p t q -> p q t"),
                     scalar=1.0,
-                    in1=inv_n[i][:, HALF * b : HALF * (b + 1)],
+                    in1=inv_n[i][:, cols].rearrange("p (q t) -> p q t", t=SUBS),
                     op0=ALU.mult,
                     op1=ALU.mult,
                     accum_out=totals[i][:, part, b : b + 1],
@@ -584,59 +604,55 @@ def tile_quantumcoherencelayer_kernel(
                 nc.sync.dma_start(out=out_rows[part][:, i, :], in_=units[i][:, part, :])
 
             def gpsimd_share(i):
-                return HALF if i < TILES - 1 else 0
+                return 2 if i < TILES - 1 else 0
 
             sine_and_cosine(0)
             count_turns(1)
             negate_first(1)
-            multiply(2)
             for step in range(0, TILES + 2):
                 if 0 <= step + 2 < TILES:
                     fetch_turned(step + 2)
                 if 0 <= step < TILES:
                     open_planes(step)
-                    product_of_vector(step, 3, slice(0, D))
-                    product_of_vector(step, 2, slice(gpsimd_share(step), D))
-                    hold_gpsimd(step)
-                    product_of_gpsimd(step, 0, slice(0, D))
-                if 0 <= step - 1 < TILES:
-                    add_products(step - 1, 1, 0)
-                    add_products(step - 1, 1, 1)
+                    imag_sine(step)
+                    imag_cosine(step)
+                if 0 <= step - 2 < TILES:
+                    open_moments(step - 2)
+                    row_moments(step - 2, slice(0, 2))
+                if 0 <= step + 2 < TILES:
+                    multiply(step + 2)
                 if 0 <= step + 1 < TILES:
                     fraction(step + 1)
+                if 0 <= step < TILES:
+                    real_product(step, 0)
+                if 0 <= step - 2 < TILES:
+                    norm_first(step - 2, 0)
+                    norm_first(step - 2, 1)
+                    inverse_deviation(step - 2, slice(0, 2))
                 if step == 1:
                     coherence_gains(GAIN_BATCH)
                 if 0 <= step + 2 < TILES:
                     count_turns(step + 2)
                 if 0 <= step - 1 < TILES:
-                    normalise(step - 1, 1, 0)
-                if 0 <= step - 2 < TILES:
-                    inverse_deviation(step - 2, slice(0, 2))
-                    norm_first(step - 2, 0)
-                if 0 <= step - 1 < TILES:
-                    normalise(step - 1, 1, 1)
-                if 0 <= step - 2 < TILES:
-                    norm_first(step - 2, 1)
-                if 0 <= step + 1 < TILES:
-                    sine_and_cosine(step + 1)
-                if 0 <= step - 1 < TILES:
-                    open_moments(step - 1)
-                    row_moments(step - 1, slice(0, 2))
+                    add_products(step - 1, 1, 0)
+                    add_products(step - 1, 1, 1)
                 if 0 <= step < TILES:
-                    product_of_gpsimd(step, 1, slice(0, D))
+                    real_product(step, 1)
                     if gpsimd_share(step) > 0:
-                        product_of_gpsimd(step, 2, slice(0, gpsimd_share(step)))
+                        imag_cosine_of_gpsimd(step)
                 if 0 <= step + 2 < TILES:
                     negate_whole(step + 2)
+                if 0 <= step - 1 < TILES:
+                    normalise(step - 1, 1, 0)
+                    normalise(step - 1, 1, 1)
                 if 0 <= step < TILES:
                     add_products(step, 0, 0)
                     add_products(step, 0, 1)
-                if 0 <= step + 3 < TILES:
-                    multiply(step + 3)
                 if 0 <= step - 2 < TILES:
                     norm_second(step - 2, 0)
+                    norm_second(step - 2, 1)
                 if 0 <= step < TILES:
                     normalise(step, 0, 0)
                     normalise(step, 0, 1)
-                if 0 <= step - 2 < TILES:
-                    norm_second(step - 2, 1)
+                if 0 <= step + 1 < TILES:
+                    sine_and_cosine(step + 1)

import math
from contextlib import ExitStack

import concourse.mybir as mybir
from concourse.masks import make_identity

F32 = mybir.dt.float32
BF16 = mybir.dt.bfloat16
I32 = mybir.dt.int32
U32 = mybir.dt.uint32
U8 = mybir.dt.uint8
FP8X4 = mybir.dt.float8_e4m3fn_x4
FP4X4 = mybir.dt.float4_e2m1fn_x4
ACT = mybir.ActivationFunctionType
ALU = mybir.AluOpType

P = 128
D = 1024
ROWS = 2 * 1024
TILES = ROWS // P
HALF = 512
BANKS = D // HALF
CHUNKS = D // P
PER_BANK = CHUNKS // BANKS
K_PASSES = D // (4 * P)
EPS = 1e-8
ROUND_MAGIC = 12582912.0
SUBS = 4
GAIN_BATCH = 8
RESIDENT = 3
PLANES = 8
SQUARE_SCALE = math.sqrt(1.0 / (2.0 * EPS))

FLOPS = 2 * ROWS * D * D


def tile_quantumcoherencelayer_kernel(
    tc,
    x_real,
    x_imag,
    phase_matrix_words,
    phase_matrix_scales,
    coherence_factor,
    ln_weight,
    ln_bias,
    out_0,
    out_1,
):
    nc = tc.nc
    xr_rows = x_real.flatten_outer_dims().rearrange("(p i) d -> p i d", i=TILES)
    xi_rows = x_imag.flatten_outer_dims().rearrange("(p i) d -> p i d", i=TILES)
    out_rows = [
        o.flatten_outer_dims().rearrange("(p i) d -> p i d", i=TILES) for o in (out_0, out_1)
    ]

    with tc.manual_schedule(), ExitStack() as whole:
        keep = whole.enter_context(tc.tile_pool(name="keep", bufs=1))
        tiny = whole.enter_context(tc.tile_pool(name="tiny", bufs=3))

        imag_words = [
            keep.tile([P, 2 * K_PASSES, P], F32, name="imag_words%d" % i) for i in range(TILES)
        ]
        inv_n = [keep.tile([P, D], F32, name="inv_n%d" % i) for i in range(TILES)]
        x_codes = [
            keep.tile([P, K_PASSES * P], U32, name="x_codes%d" % i, align_bytes=64)
            for i in range(TILES)
        ]
        x_scales = [
            keep.tile([P, K_PASSES * P], U8, name="x_scales%d" % i, align_bytes=64)
            for i in range(TILES)
        ]
        phase_sums = keep.tile([P, TILES, 2, BANKS], F32, name="phase_sums")
        turns_gain = keep.tile([P, TILES], F32, name="turns_gain")

        psum = whole.enter_context(tc.psum_pool(name="psum", bufs=2))
        affine = psum.tile([P, 2, D], BF16, name="affine", bufs=1)
        turns = [
            [keep.tile([P, BANKS, SUBS, P], F32, name="turns%d%d" % (turn, which)) for which in range(2)]
            for turn in range(2)
        ]
        products = {}
        fractions = {}

        keep_ring = whole.enter_context(tc.tile_pool(name="keep_ring", bufs=RESIDENT))
        real_turned = {}

        x_tiles = {}
        words = {}
        grouped_words = {}
        squares = {}
        part_sums = {}
        square_sums = {}
        radii = {}
        inv_r_turned = {}
        inv_r = {}

        with tc.tile_pool(name="x_in", bufs=5) as x_in, tc.tile_pool(
            name="work1", bufs=2
        ) as work1:

            def load(i):
                xri = x_in.tile([P, 2, D], BF16, name="xri")
                nc.sync.dma_start(out=xri[:, 0, :], in_=xr_rows[:, i, :])
                nc.sync.dma_start(out=xri[:, 1, :], in_=xi_rows[:, i, :])
                x_tiles[i] = xri

            load(0)
            load(1)

            ident = keep.tile([P, P], F32, name="ident")
            make_identity(nc, ident[:])
            ones = keep.tile([P, 1], F32, name="ones")
            nc.vector.memset(ones[:], 1.0)
            eps = keep.tile([P, 1], F32, name="eps")
            nc.vector.tensor_scalar(
                out=eps[:], in0=ones[:], scalar1=EPS, scalar2=None, op0=ALU.mult
            )
            two_eps_sq = keep.tile([P, 1], F32, name="two_eps_sq")
            nc.vector.tensor_scalar(
                out=two_eps_sq[:], in0=ones[:], scalar1=2.0 * EPS * EPS, scalar2=None, op0=ALU.mult
            )
            quarter_turn = keep.tile([P, 1], F32, name="quarter_turn")
            nc.vector.tensor_scalar(
                out=quarter_turn[:], in0=ones[:], scalar1=math.pi / 2, scalar2=None, op0=ALU.mult
            )
            magic = keep.tile([P, 1], F32, name="magic")
            nc.vector.memset(magic[:], ROUND_MAGIC)
            minus_half = keep.tile([P, 2], F32, name="minus_half")
            nc.vector.memset(minus_half[:], -0.5)
            warm_up = keep.tile([P, 1], F32, name="warm_up")
            nc.scalar.activation(out=warm_up[:], in_=ones[:], func=ACT.Abs_reciprocal_sqrt)

            w_words = keep.tile([P, K_PASSES, 2 * D], U8, name="w_words", align_bytes=64)
            w_scales = keep.tile([P, K_PASSES, D], U8, name="w_scales", align_bytes=64)
            nc.vector.memset(w_scales[:].bitcast(I32), 0)
            factor = keep.tile([P, 1], BF16, name="factor")
            nc.sync.dma_start(out=factor[:], in_=coherence_factor.partition_broadcast(P))
            for quadrant in range(4):
                nc.sync.dma_start(
                    out=w_scales[32 * quadrant : 32 * quadrant + 4, :, :].bitcast(I32),
                    in_=phase_matrix_scales[:, 4 * quadrant : 4 * quadrant + 4, :]
                    .rearrange("g r n -> r g n")
                    .bitcast(I32),
                )
            nc.sync.dma_start(
                out=w_words[:].bitcast(I32),
                in_=phase_matrix_words.rearrange("g p n -> p g n").bitcast(I32),
            )
            full_gain = keep.tile([P, 1], F32, name="full_gain")
            nc.vector.tensor_scalar(
                out=full_gain[:],
                in0=factor[:],
                scalar1=1.0 / (2.0 * math.pi),
                scalar2=None,
                op0=ALU.mult,
            )
            gain_slope = keep.tile([P, 1], F32, name="gain_slope")
            nc.vector.tensor_scalar(
                out=gain_slope[:],
                in0=factor[:],
                scalar1=-1.0 / (2.0 * math.pi * D * D),
                scalar2=None,
                op0=ALU.mult,
            )

            ln_rows = work1.tile([P, 2, D], BF16, name="ln_rows", bufs=1)
            nc.gpsimd.memset(ln_rows[:], 0.0)
            nc.sync.dma_start(out=ln_rows[0:1, 0, :], in_=ln_weight.rearrange("(o d) -> o d", o=1))
            nc.sync.dma_start(out=ln_rows[0:1, 1, :], in_=ln_bias.rearrange("(o d) -> o d", o=1))
            first_row = work1.tile([P, P], BF16, name="first_row", bufs=1)
            nc.gpsimd.memset(first_row[:], 0.0)
            nc.gpsimd.memset(first_row[0:1, :], 1.0)
            def spread_affine():
                for which in range(2):
                    for b in range(BANKS):
                        nc.tensor.matmul(
                            out=affine[:, which, HALF * b : HALF * (b + 1)],
                            lhsT=first_row[:],
                            rhs=ln_rows[:, which, HALF * b : HALF * (b + 1)],
                            start=True,
                            stop=True,
                        )

            def turn_words(i):
                for part in range(2):
                    x_words = x_tiles[i][:, part, :].bitcast(F32)
                    xt = psum.tile([P, 2 * K_PASSES, P], F32, name="ring_a")
                    for g in range(K_PASSES):
                        for u in range(2):
                            nc.tensor.transpose(
                                xt[:, 2 * g + u, :], x_words[:, 256 * g + u : 256 * (g + 1) : 2], ident[:]
                            )
                    words[i, part] = xt

            def group_words(i):
                grouped = work1.tile([P, K_PASSES, P, 2], F32, name="grouped", align_bytes=64)
                nc.scalar.copy(
                    out=grouped[:], in_=words[i, 0][:].rearrange("p (g u) r -> p g r u", u=2)
                )
                grouped_words[i] = grouped

            def halves(tile):
                return tile[:].bitcast(BF16).rearrange("p w (r h) -> p w h r", h=2)

            def by_half(plane):
                return plane.rearrange("p (w h r) -> p w h r", h=2, r=P)

            def keep_turned(i):
                resident = i < RESIDENT
                turned = (keep_ring if resident else work1).tile([P, D], F32, name="real_turned")
                nc.vector.tensor_copy(
                    out=by_half(turned[:]),
                    in_=halves(words[i, 0]),
                )
                if resident:
                    real_turned[i] = turned
                else:
                    nc.sync.dma_start(out=out_rows[0][:, i, :], in_=turned[:])
                nc.vector.tensor_copy(out=imag_words[i][:], in_=words[i, 1][:])

            def quantise(i):
                nc.vector.quantize_mx(
                    out=x_codes[i][:].bitcast(FP8X4),
                    scales=x_scales[i][:],
                    in_=grouped_words[i][:].rearrange("p g r u -> p (g r u)").bitcast(BF16),
                )

            def square(i):
                sq = work1.tile([P, 2, D], F32, name="sq")
                nc.scalar.activation(
                    out=sq[:], in_=x_tiles[i][:], func=ACT.Square, scale=SQUARE_SCALE
                )
                squares[i] = sq

            def add_parts(i):
                part_sum = work1.tile([P, D], F32, name="part_sum")
                nc.gpsimd.tensor_tensor(
                    out=part_sum[:], in0=x_tiles[i][:, 0, :], in1=x_tiles[i][:, 1, :], op=ALU.add
                )
                part_sums[i] = part_sum
                square_sum = work1.tile([P, D], F32, name="square_sum")
                nc.gpsimd.tensor_tensor(
                    out=square_sum[:], in0=squares[i][:, 0, :], in1=squares[i][:, 1, :], op=ALU.add
                )
                square_sums[i] = square_sum

            def root_n(i):
                nc.scalar.activation(
                    out=inv_n[i][:],
                    in_=square_sums[i][:],
                    func=ACT.Abs_reciprocal_sqrt,
                    scale=2.0 * EPS,
                    bias=eps[:],
                )

            def add_shift(i):
                for b in range(BANKS):
                    radius = psum.tile([P, PER_BANK, P], F32, name="ring_b")
                    for c in range(PER_BANK):
                        cols = slice(P * (PER_BANK * b + c), P * (PER_BANK * b + c + 1))
                        for which, addend in enumerate((square_sums[i], part_sums[i])):
                            nc.tensor.matmul(
                                out=radius[:, c, :],
                                lhsT=addend[:, cols],
                                rhs=ident[:],
                                is_transpose=True,
                                start=(which == 0),
                                stop=(which == 1),
                            )
                    radii[i, b] = radius

            def root_r(i):
                turned = work1.tile([P, CHUNKS, P], F32, name="inv_r_turned")
                for b in range(BANKS):
                    nc.scalar.activation(
                        out=turned[:, PER_BANK * b : PER_BANK * (b + 1), :],
                        in_=radii[i, b][:],
                        func=ACT.Abs_reciprocal_sqrt,
                        scale=2.0 * EPS,
                        bias=two_eps_sq[:],
                    )
                inv_r_turned[i] = turned

            def turn_back(i):
                for b in range(BANKS):
                    rows = psum.tile([P, HALF], F32, name="ring_c")
                    for c in range(PER_BANK):
                        nc.tensor.transpose(
                            rows[:, P * c : P * (c + 1)],
                            inv_r_turned[i][:, PER_BANK * b + c, :],
                            ident[:],
                        )
                    inv_r[i, b] = rows

            def add_phases(i):
                for b in range(BANKS):
                    for part in range(2):
                        unread = work1.tile([P, HALF], F32, name="unread")
                        nc.vector.scalar_tensor_tensor(
                            out=unread[:],
                            in0=x_tiles[i][:, part, HALF * b : HALF * (b + 1)],
                            scalar=EPS,
                            in1=inv_r[i, b][:],
                            op0=ALU.add,
                            op1=ALU.mult,
                            accum_out=phase_sums[:, i, part, b : b + 1],
                        )

            def coherence_gains(first):
                batch = slice(first, first + GAIN_BATCH)
                sums = tiny.tile([P, GAIN_BATCH, 2], F32, name="sums", bufs=1)
                nc.gpsimd.tensor_tensor(
                    out=sums[:], in0=phase_sums[:, batch, :, 0], in1=phase_sums[:, batch, :, 1], op=ALU.add
                )
                sums_sq = tiny.tile([P, GAIN_BATCH, 2], F32, name="sums_sq", bufs=1)
                nc.gpsimd.tensor_tensor(out=sums_sq[:], in0=sums[:], in1=sums[:], op=ALU.mult)
                length_sq = tiny.tile([P, GAIN_BATCH], F32, name="length_sq", bufs=1)
                nc.gpsimd.tensor_tensor(
                    out=length_sq[:], in0=sums_sq[:, :, 0], in1=sums_sq[:, :, 1], op=ALU.add
                )
                nc.gpsimd.tensor_scalar(
                    out=turns_gain[:, batch],
                    in0=length_sq[:],
                    scalar1=gain_slope[:],
                    scalar2=full_gain[:],
                    op0=ALU.mult,
                    op1=ALU.add,
                )

            def multiply(i):
                for b in range(BANKS):
                    product = psum.tile([P, HALF], F32, name="ring_a")
                    for g in range(K_PASSES):
                        nc.tensor.matmul_mx(
                            out=product[:],
                            lhsT=x_codes[i][:, P * g : P * (g + 1)].bitcast(FP8X4),
                            lhsT_scale=x_scales[i][:, P * g : P * (g + 1)],
                            rhs=w_words[:, g, 2 * HALF * b : 2 * HALF * (b + 1)].bitcast(FP4X4),
                            rhs_scale=w_scales[:, g, HALF * b : HALF * (b + 1)],
                            start=(g == 0),
                            stop=(g == K_PASSES - 1),
                        )
                    products[i, b] = product

            def count_turns(i):
                angle, whole = turns[i % 2]
                for b in range(BANKS):
                    by_sub = products[i, b][:].rearrange("p (q t) -> p q t", t=SUBS)
                    nc.scalar.activation(
                        out=angle[:, b].rearrange("p t q -> p q t"), in_=by_sub, func=ACT.Copy, scale=turns_gain[:, i : i + 1]
                    )
                    nc.scalar.activation(
                        out=whole[:, b].rearrange("p t q -> p q t"),
                        in_=by_sub,
                        func=ACT.Identity,
                        scale=turns_gain[:, i : i + 1],
                        bias=magic[:],
                    )

            def negate_first(i):
                whole = turns[i % 2][1]
                nc.scalar.activation(
                    out=whole[:], in_=whole[:], func=ACT.Identity, scale=-1.0, bias=magic[:]
                )

            def negate_whole(i):
                whole = turns[i % 2][1]
                nc.gpsimd.tensor_scalar(
                    out=whole[:],
                    in0=whole[:],
                    scalar1=-1.0,
                    scalar2=ROUND_MAGIC,
                    op0=ALU.mult,
                    op1=ALU.add,
                )

            def fraction(i):
                for b in range(BANKS):
                    frac = psum.tile([P, SUBS, P], F32, name="ring_b")
                    for t in range(SUBS):
                        for which in range(2):
                            nc.tensor.matmul(
                                out=frac[:, t, :],
                                lhsT=turns[i % 2][which][:, b, t, :],
                                rhs=ident[:],
                                is_transpose=True,
                                start=(which == 0),
                                stop=(which == 1),
                            )
                    fractions[i, b] = frac

            for step in range(TILES + 2):
                if step + 2 < TILES:
                    load(step + 2)
                if 0 <= step - 1 < TILES:
                    add_shift(step - 1)
                if 0 <= step - 2:
                    turn_back(step - 2)
                if step == TILES - 1:
                    multiply(0)
                if step < TILES:
                    square(step)
                    add_parts(step)
                if step < TILES:
                    turn_words(step)
                if 0 <= step - 1 < TILES:
                    root_n(step - 1)
                    root_r(step - 1)
                if step == TILES - 1:
                    count_turns(0)
                if 0 <= step - 1 < TILES:
                    quantise(step - 1)
                if step == TILES:
                    negate_whole(0)
                if 0 <= step - 2:
                    add_phases(step - 2)
                if step < TILES:
                    group_words(step)
                    keep_turned(step)
                if step == GAIN_BATCH + 1:
                    coherence_gains(0)
                if step == TILES:
                    nc.scalar.activation(out=warm_up[:], in_=ones[:], func=ACT.Sin)
                    fraction(0)
                if step == TILES + 1:
                    multiply(1)
                if step == GAIN_BATCH:
                    spread_affine()

        with tc.tile_pool(name="late", bufs=4, reuse_waits="tile") as late, tc.tile_pool(
            name="work2", bufs=2, reuse_waits="tile"
        ) as work2:
            phasors = {}
            planes = {}
            rotated = {}
            rotated_rows = {}
            units = {}
            totals = {}
            moments = {}

            def sine_and_cosine(i):
                phasor = work2.tile([P, 2, D], F32, name="phasor")
                for b in range(BANKS):
                    turn = fractions[i, b][:].rearrange("p t r -> p (t r)")
                    cols = slice(HALF * b, HALF * (b + 1))
                    nc.scalar.activation(out=phasor[:, 0, cols], in_=turn, func=ACT.Abs)
                    nc.scalar.activation(
                        out=phasor[:, 1, cols], in_=turn, func=ACT.Sin, scale=2.0 * math.pi
                    )
                nc.scalar.activation(
                    out=phasor[:, 0],
                    in_=phasor[:, 0],
                    func=ACT.Sin,
                    scale=-2.0 * math.pi,
                    bias=quarter_turn[:],
                )
                phasors[i] = phasor

            def open_planes(i):
                for which in (3, 0, 1, 2):
                    planes[i, which] = work2.tile([P, D], F32, name="plane", bufs=PLANES)
                rotated[i] = ((planes[i, 0], planes[i, 3]), (planes[i, 1], planes[i, 2]))

            def fetch_turned(i):
                if i >= RESIDENT:
                    real_turned[i] = keep_ring.tile([P, D], F32, name="real_turned")
                    nc.sync.dma_start(out=real_turned[i][:], in_=out_rows[0][:, i, :])

            def real_product(i, which):
                nc.gpsimd.tensor_tensor(
                    out=planes[i, which][:],
                    in0=real_turned[i][:],
                    in1=phasors[i][:, which, :],
                    op=ALU.mult,
                )

            def imag_cosine_of_gpsimd(i):
                mine = slice(0, gpsimd_share(i))
                nc.gpsimd.tensor_tensor(
                    out=by_half(planes[i, 2][:])[:, mine],
                    in0=halves(imag_words[i])[:, mine],
                    in1=by_half(phasors[i][:, 0, :])[:, mine],
                    op=ALU.mult,
                )

            def imag_cosine(i):
                mine = slice(gpsimd_share(i), 2 * K_PASSES)
                nc.vector.tensor_tensor(
                    out=by_half(planes[i, 2][:])[:, mine],
                    in0=halves(imag_words[i])[:, mine],
                    in1=by_half(phasors[i][:, 0, :])[:, mine],
                    op=ALU.mult,
                )

            def imag_sine(i):
                for h in range(2):
                    nc.vector.scalar_tensor_tensor(
                        out=by_half(planes[i, 3][:])[:, :, h, :],
                        in0=halves(imag_words[i])[:, :, h, :],
                        scalar=-1.0,
                        in1=by_half(phasors[i][:, 1, :])[:, :, h, :],
                        op0=ALU.mult,
                        op1=ALU.mult,
                    )

            def hold_gpsimd(i):
                nc.vector.memset(planes[i, 0][:, 0:1], 0.0)

            def add_products(i, part, b):
                rows = psum.tile([P, SUBS, P], F32, name="ring_c")
                for t in range(SUBS):
                    for which in range(2):
                        nc.tensor.matmul(
                            out=rows[:, t, :],
                            lhsT=rotated[i][part][which][:, HALF * b + P * t : HALF * b + P * (t + 1)],
                            rhs=ident[:],
                            is_transpose=True,
                            start=(which == 0),
                            stop=(which == 1),
                        )
                rotated_rows[i, part, b] = rows

            def normalise(i, part, b):
                if (part, b) == (0, 0):
                    units[i] = late.tile([P, 2, D], F32, name="unit")
                    totals[i] = tiny.tile([P, 2, BANKS], F32, name="total")
                cols = slice(HALF * b, HALF * (b + 1))
                nc.vector.scalar_tensor_tensor(
                    out=units[i][:, part, cols].rearrange("p (q t) -> p q t", t=SUBS),
                    in0=rotated_rows[i, part, b][:].rearrange("p t q -> p q t"),
                    scalar=1.0,
                    in1=inv_n[i][:, cols].rearrange("p (q t) -> p q t", t=SUBS),
                    op0=ALU.mult,
                    op1=ALU.mult,
                    accum_out=totals[i][:, part, b : b + 1],
                )

            def open_moments(i):
                moments[i] = [tiny.tile([P, 2], F32, name=name) for name in ("mean", "spread", "rstd")]

            def row_moments(i, parts):
                mean, spread = moments[i][0:2]
                shares = tiny.tile([P, 2, BANKS], F32, name="shares")
                nc.scalar.activation(
                    out=shares[:, parts, :], in_=totals[i][:, parts, :], func=ACT.Copy, scale=1.0 / D
                )
                each = range(parts.start, parts.stop)
                for part in each:
                    nc.scalar.activation(
                        out=mean[:, part : part + 1],
                        in_=shares[:, part, 0:1],
                        func=ACT.Identity,
                        bias=shares[:, part, 1:2],
                    )
                total_sq = tiny.tile([P, 2], F32, name="total_sq")
                for part in each:
                    unread = work2.tile([P, D], BF16, name="unread_sq", bufs=1)
                    nc.scalar.activation(
                        out=unread[:],
                        in_=units[i][:, part, :],
                        func=ACT.Square,
                        accum_out=total_sq[:, part : part + 1],
                    )
                mean_sq = tiny.tile([P, 2], F32, name="mean_sq")
                nc.scalar.activation(out=mean_sq[:, parts], in_=mean[:, parts], func=ACT.Square)
                shift = tiny.tile([P, 2], F32, name="shift")
                nc.scalar.activation(
                    out=shift[:, parts], in_=mean_sq[:, parts], func=ACT.Identity, scale=-1.0, bias=eps[:]
                )
                for part in each:
                    nc.scalar.activation(
                        out=spread[:, part : part + 1],
                        in_=total_sq[:, part : part + 1],
                        func=ACT.Identity,
                        scale=1.0 / D,
                        bias=shift[:, part : part + 1],
                    )

            def inverse_deviation(i, parts):
                mean, spread, rstd = moments[i]
                nc.gpsimd.tensor_tensor(
                    out=rstd[:, parts], in0=spread[:, parts], in1=minus_half[:, parts], op=ALU.pow
                )

            def norm_first(i, part):
                nc.vector.scalar_tensor_tensor(
                    out=units[i][:, part, :],
                    in0=units[i][:, part, :],
                    scalar=moments[i][0][:, part : part + 1],
                    in1=affine[:, 0, :],
                    op0=ALU.subtract,
                    op1=ALU.mult,
                )

            def norm_second(i, part):
                nc.vector.scalar_tensor_tensor(
                    out=units[i][:, part, :],
                    in0=units[i][:, part, :],
                    scalar=moments[i][2][:, part : part + 1],
                    in1=affine[:, 1, :],
                    op0=ALU.mult,
                    op1=ALU.add,
                )
                nc.sync.dma_start(out=out_rows[part][:, i, :], in_=units[i][:, part, :])

            def gpsimd_share(i):
                return 2 if i < TILES - 1 else 0

            sine_and_cosine(0)
            count_turns(1)
            negate_first(1)
            for step in range(0, TILES + 2):
                if 0 <= step + 2 < TILES:
                    fetch_turned(step + 2)
                if 0 <= step < TILES:
                    open_planes(step)
                    imag_sine(step)
                    imag_cosine(step)
                if 0 <= step - 2 < TILES:
                    open_moments(step - 2)
                    row_moments(step - 2, slice(0, 2))
                if 0 <= step + 2 < TILES:
                    multiply(step + 2)
                if 0 <= step + 1 < TILES:
                    fraction(step + 1)
                if 0 <= step < TILES:
                    real_product(step, 0)
                if 0 <= step - 2 < TILES:
                    norm_first(step - 2, 0)
                    norm_first(step - 2, 1)
                    inverse_deviation(step - 2, slice(0, 2))
                if step == 1:
                    coherence_gains(GAIN_BATCH)
                if 0 <= step + 2 < TILES:
                    count_turns(step + 2)
                if 0 <= step - 1 < TILES:
                    add_products(step - 1, 1, 0)
                    add_products(step - 1, 1, 1)
                if 0 <= step < TILES:
                    real_product(step, 1)
                    if gpsimd_share(step) > 0:
                        imag_cosine_of_gpsimd(step)
                if 0 <= step + 2 < TILES:
                    negate_whole(step + 2)
                if 0 <= step - 1 < TILES:
                    normalise(step - 1, 1, 0)
                    normalise(step - 1, 1, 1)
                if 0 <= step < TILES:
                    add_products(step, 0, 0)
                    add_products(step, 0, 1)
                if 0 <= step - 2 < TILES:
                    norm_second(step - 2, 0)
                    norm_second(step - 2, 1)
                if 0 <= step < TILES:
                    normalise(step, 0, 0)
                    normalise(step, 0, 1)
                if 0 <= step + 1 < TILES:
                    sine_and_cosine(step + 1)
